import numpy as np
import ml_dtypes


def mxq(x, axis, fmt="e4m3"):
    dtype, down = {"e4m3": (ml_dtypes.float8_e4m3fn, 7), "e5m2": (ml_dtypes.float8_e5m2, 14)}[fmt]
    v = np.moveaxis(np.asarray(x, np.float32).astype(ml_dtypes.bfloat16).astype(np.float64), axis, -1)
    blocks = v.reshape(v.shape[:-1] + (-1, 32))
    amax = np.abs(blocks).max(-1, keepdims=True)
    byte = np.maximum(np.where(amax > 0, np.frexp(amax)[1] - 1 + 127, 0) - down, 1)
    scale = np.exp2(byte - 127.0)
    codes = (blocks / scale).astype(np.float32).astype(dtype).astype(np.float64)
    return np.moveaxis((codes * scale).reshape(v.shape), -1, axis)


WIDE = False


def mx_kscale(k):
    if not WIDE:
        return np.ones(k)
    levels = np.array([10, -10, 5, -5, 0])
    a = np.random.permutation(np.resize(levels, k // 512 * 4)).reshape(k // 512, 4)
    idx = np.arange(k)
    return np.exp2(a[idx // 512, idx % 128 // 32])


BF16 = ml_dtypes.bfloat16


def bf(x):
    return np.asarray(x, np.float32).astype(BF16)


def f64(x):
    return np.asarray(x).astype(np.float64)


B, N, D, H, DK, DV = 4, 1024, 512, 8, 64, 64


def xnorm(x, g):
    n = np.sqrt(np.sum(x * x, axis=-1, keepdims=True))
    return x * g / n


def setup_inputs():
    s = mx_kscale(D)
    return {
        "queries": bf(np.random.standard_normal((B, N, D)) * s),
        "Wk": bf(np.random.standard_normal((D, H * DK)) * 0.5 / np.sqrt(D) / s[:, None]),
        "bk": bf(np.random.standard_normal(H * DK) * 0.05),
        "Wv": bf(np.random.standard_normal((D, H * DV)) * 0.5 / np.sqrt(D) / s[:, None]),
        "bv": bf(np.random.standard_normal(H * DV) * 0.05),
        "gamma": bf(np.random.standard_normal((1, H, 1, 1)) * 2.0),
    }


def reference(queries, Wk, bk, Wv, bv, gamma):
    xq = mxq(f64(queries), 2, "e4m3")
    k = ((xq @ mxq(f64(Wk), 0, "e4m3")) + f64(bk)).reshape(B, N, H, DK)
    v = ((xq @ mxq(f64(Wv), 0, "e4m3")) + f64(bv)).reshape(B, N, H, DV)
    kv = mxq(k.transpose(0, 2, 3, 1), 3, "e4m3") @ mxq(v.transpose(0, 2, 1, 3), 2, "e4m3")
    return xnorm(kv, f64(gamma))

@@ -1,0 +1,201 @@
+from contextlib import ExitStack
+
+import concourse.mybir as mybir
+from concourse.masks import make_identity
+
+F32 = mybir.dt.float32
+BF16 = mybir.dt.bfloat16
+U32 = mybir.dt.uint32
+U8 = mybir.dt.uint8
+FP8X4 = mybir.dt.float8_e4m3fn_x4
+ACT = mybir.ActivationFunctionType
+
+P = 128
+PACK = 4
+K_PASS = P * PACK
+
+BATCHES = 4
+TOKENS = 1024
+D_MODEL = 512
+HEADS = 8
+D_HEAD = 64
+FEATURES = HEADS * D_HEAD
+
+GROUPS = BATCHES * TOKENS // K_PASS
+GROUPS_PER_BATCH = TOKENS // K_PASS
+FEATURE_TILES = 2 * FEATURES // P
+HEAD_PAIRS = FEATURES // P
+
+FLOPS = 2 * BATCHES * TOKENS * D_MODEL * 2 * FEATURES + 2 * BATCHES * HEADS * TOKENS * D_HEAD * D_HEAD
+
+assert D_MODEL == K_PASS
+
+
+def tile_ufoattention_pa_kernel(tc, queries, Wk, bk, Wv, bv, gamma, out):
+    nc = tc.nc
+    with ExitStack() as ctx:
+        consts = ctx.enter_context(tc.tile_pool(name="consts", bufs=1))
+        x_pool = ctx.enter_context(tc.tile_pool(name="x", bufs=GROUPS))
+        xt_pool = ctx.enter_context(tc.tile_pool(name="xt", bufs=2))
+        kv_pool = ctx.enter_context(tc.tile_pool(name="kv", bufs=2))
+        kvq_pool = ctx.enter_context(tc.tile_pool(name="kvq", bufs=2 * GROUPS_PER_BATCH))
+        end_pool = ctx.enter_context(tc.tile_pool(name="end", bufs=2))
+        xt_psum = ctx.enter_context(tc.psum_pool(name="xt_psum", bufs=2))
+        proj_psum = ctx.enter_context(tc.psum_pool(name="proj_psum", bufs=5))
+        kv_psum = ctx.enter_context(tc.psum_pool(name="kv_psum", bufs=1))
+
+        x_groups = queries.flatten_outer_dims().rearrange("(g p j) d -> g p (j d)", p=P, j=PACK)
+        x_tiles = []
+        w_raw = []
+        for g in range(GROUPS):
+            x_sb = x_pool.tile([P, PACK * D_MODEL], BF16, name="x_sb")
+            nc.sync.dma_start(out=x_sb[:], in_=x_groups[g])
+            x_tiles.append(x_sb)
+            if g == 0:
+                for w_name, w in (("wk_raw", Wk), ("wv_raw", Wv)):
+                    raw = consts.tile([P, PACK, FEATURES], BF16, name=w_name)
+                    nc.sync.dma_start(out=raw[:], in_=w.rearrange("(p t) n -> p t n", t=PACK))
+                    w_raw.append(raw)
+
+        ident = consts.tile([P, P], F32, name="ident")
+        make_identity(nc, ident[:])
+
+        bias_row = consts.tile([P, 2 * FEATURES], BF16, name="bias_row")
+        nc.vector.memset(bias_row[:], 0.0)
+        nc.scalar.dma_start(out=bias_row[0:1, 0:FEATURES], in_=bk.rearrange("(o n) -> o n", o=1))
+        nc.scalar.dma_start(out=bias_row[0:1, FEATURES : 2 * FEATURES], in_=bv.rearrange("(o n) -> o n", o=1))
+        ones = consts.tile([P, P], BF16, name="ones")
+        nc.vector.memset(ones[:], 1.0)
+
+        gamma_all = consts.tile([P, HEADS], BF16, name="gamma_all")
+        nc.scalar.dma_start(out=gamma_all[:], in_=gamma.rearrange("a h b c -> (a h b c)").partition_broadcast(P))
+        gamma_by_half = gamma_all[:].rearrange("p (pair half) -> p half pair", half=2)
+        gain = consts.tile([P, HEAD_PAIRS], F32, name="gain")
+        nc.vector.tensor_copy(out=gain[0:D_HEAD, :], in_=gamma_by_half[0:D_HEAD, 0, :])
+        nc.vector.tensor_copy(out=gain[D_HEAD:P, :], in_=gamma_by_half[D_HEAD:P, 1, :])
+
+        def transpose_group(g):
+            xt_grouped = xt_pool.tile([P, PACK * K_PASS], BF16, name="xt_grouped", align_bytes=64)
+            x_words = x_tiles[g][:].bitcast(F32).rearrange("p (j q u) -> p j u q", j=PACK, u=2)
+            grouped_words = xt_grouped[:].bitcast(F32).rearrange("q (m u) -> q m u", u=2)
+            for half in range(2):
+                xt_bank = xt_psum.tile([P, 2, 2 * P], F32, name="xt_bank")
+                for jj in range(2):
+                    for u in range(2):
+                        nc.tensor.transpose(
+                            xt_bank[:, u, jj * P : (jj + 1) * P], x_words[:, 2 * half + jj, u, :], ident[:]
+                        )
+                nc.scalar.copy(
+                    out=grouped_words[:, half * 2 * P : (half + 1) * 2 * P, :],
+                    in_=xt_bank[:].rearrange("q u m -> q m u"),
+                )
+            return xt_grouped
+
+        def quantise_x(xt_grouped):
+            x_codes = xt_pool.tile([P, K_PASS], U32, name="x_codes", align_bytes=64)
+            x_scales = xt_pool.tile([P, K_PASS], U8, name="x_scales", align_bytes=64)
+            nc.vector.quantize_mx(out=x_codes[:].bitcast(FP8X4), scales=x_scales[:], in_=xt_grouped[:])
+            return x_codes, x_scales
+
+        x_quantised = quantise_x(transpose_group(0))
+
+        w_codes = consts.tile([P, 2 * FEATURES], U32, name="w_codes", align_bytes=64)
+        w_scales = consts.tile([P, 2 * FEATURES], U8, name="w_scales", align_bytes=64)
+        for i, w_name in enumerate(("wk_grouped", "wv_grouped")):
+            w_grouped = consts.tile([P, FEATURES, PACK], BF16, name=w_name, align_bytes=64)
+            nc.vector.tensor_copy(out=w_grouped[:], in_=w_raw[i][:].rearrange("p t n -> p n t"))
+            cols = slice(i * FEATURES, (i + 1) * FEATURES)
+            nc.vector.quantize_mx(
+                out=w_codes[:, cols].bitcast(FP8X4),
+                scales=w_scales[:, cols],
+                in_=w_grouped[:].rearrange("p n t -> p (n t)"),
+            )
+
+        bias = consts.tile([P, 2 * FEATURES], F32, name="bias")
+        for i in range(2):
+            cols = slice(i * FEATURES, (i + 1) * FEATURES)
+            bias_bank = proj_psum.tile([P, FEATURES], F32, name="bias_bank", tag="proj_bank")
+            nc.tensor.matmul(out=bias_bank[:], lhsT=ones[:], rhs=bias_row[:, cols], start=True, stop=True)
+            nc.scalar.copy(out=bias[:, cols], in_=bias_bank[:])
+
+        def finish_batch(b, kv_quantised):
+            kv_bank = kv_psum.tile([P, HEAD_PAIRS, P], F32, name="kv_bank")
+            for pair in range(HEAD_PAIRS):
+                k_cols = slice(pair * P, (pair + 1) * P)
+                v_cols = slice(FEATURES + pair * P, FEATURES + (pair + 1) * P)
+                for c, (codes, scales) in enumerate(kv_quantised):
+                    nc.tensor.matmul_mx(
+                        out=kv_bank[:, pair, :],
+                        lhsT=codes[:, k_cols].bitcast(FP8X4),
+                        lhsT_scale=scales[:, k_cols],
+                        rhs=codes[:, v_cols].bitcast(FP8X4),
+                        rhs_scale=scales[:, v_cols],
+                        start=(c == 0),
+                        stop=(c == GROUPS_PER_BATCH - 1),
+                    )
+            kv = end_pool.tile([P, HEAD_PAIRS, D_HEAD], F32, name="kv")
+            for half in range(2):
+                rows = slice(half * D_HEAD, (half + 1) * D_HEAD)
+                nc.scalar.copy(out=kv[rows, :, :], in_=kv_bank[rows, :, half * D_HEAD : (half + 1) * D_HEAD])
+            squares = end_pool.tile([P, HEAD_PAIRS, D_HEAD], F32, name="squares")
+            sum_squares = end_pool.tile([P, HEAD_PAIRS], F32, name="sum_squares")
+            for pair in range(HEAD_PAIRS):
+                nc.scalar.activation(
+                    out=squares[:, pair, :],
+                    in_=kv[:, pair, :],
+                    func=ACT.Square,
+                    accum_out=sum_squares[:, pair : pair + 1],
+                )
+            norm = end_pool.tile([P, HEAD_PAIRS], F32, name="norm")
+            nc.scalar.activation(out=norm[:], in_=sum_squares[:], func=ACT.Sqrt)
+            factor = end_pool.tile([P, HEAD_PAIRS], F32, name="factor")
+            nc.vector.reciprocal(out=factor[:], in_=norm[:])
+            nc.vector.tensor_mul(out=factor[:], in0=factor[:], in1=gain[:])
+            result = end_pool.tile([P, HEAD_PAIRS, D_HEAD], F32, name="result")
+            for pair in range(HEAD_PAIRS):
+                nc.scalar.activation(
+                    out=result[:, pair, :], in_=kv[:, pair, :], func=ACT.Copy, scale=factor[:, pair : pair + 1]
+                )
+            nc.sync.dma_start(
+                out=out[b].rearrange("(pair half) i j -> (half i) pair j", half=2), in_=result[:]
+            )
+
+        kv_quantised = []
+        for g in range(GROUPS):
+            if g + 1 < GROUPS:
+                xt_next = transpose_group(g + 1)
+            x_codes, x_scales = x_quantised
+            kv_grouped = kv_pool.tile([P, FEATURE_TILES, P, PACK], BF16, name="kv_grouped", align_bytes=64)
+            for f in range(FEATURE_TILES):
+                f_cols = slice(f * P, (f + 1) * P)
+                proj_bank = proj_psum.tile([P, PACK, P], F32, name="proj_bank")
+                for j in range(PACK):
+                    j_cols = slice(j * P, (j + 1) * P)
+                    nc.tensor.matmul_mx(
+                        out=proj_bank[:, j, :],
+                        lhsT=x_codes[:, j_cols].bitcast(FP8X4),
+                        lhsT_scale=x_scales[:, j_cols],
+                        rhs=w_codes[:, f_cols].bitcast(FP8X4),
+                        rhs_scale=w_scales[:, f_cols],
+                        start=True,
+                        stop=True,
+                    )
+                nc.vector.tensor_tensor(
+                    out=kv_grouped[:, f, :, :],
+                    in0=proj_bank[:].rearrange("p j w -> p w j"),
+                    in1=bias[:, f_cols].unsqueeze(2).to_broadcast([P, P, PACK]),
+                    op=mybir.AluOpType.add,
+                )
+                if f == FEATURE_TILES // 2 - 1 and g + 1 < GROUPS:
+                    x_quantised = quantise_x(xt_next)
+            kv_codes = kvq_pool.tile([P, 2 * FEATURES], U32, name="kv_codes", align_bytes=64)
+            kv_scales = kvq_pool.tile([P, 2 * FEATURES], U8, name="kv_scales", align_bytes=64)
+            nc.vector.quantize_mx(
+                out=kv_codes[:].bitcast(FP8X4),
+                scales=kv_scales[:],
+                in_=kv_grouped[:].rearrange("p f w j -> p (f w j)"),
+            )
+            kv_quantised.append((kv_codes, kv_scales))
+            if len(kv_quantised) == GROUPS_PER_BATCH:
+                finish_batch(g // GROUPS_PER_BATCH, kv_quantised)
+                kv_quantised = []

@@ -9,6 +9,7 @@ U32 = mybir.dt.uint32
 U8 = mybir.dt.uint8
 FP8X4 = mybir.dt.float8_e4m3fn_x4
 ACT = mybir.ActivationFunctionType
+ADD = mybir.AluOpType.add
 
 P = 128
 PACK = 4
@@ -26,6 +27,8 @@ GROUPS_PER_BATCH = TOKENS // K_PASS
 FEATURE_TILES = 2 * FEATURES // P
 HEAD_PAIRS = FEATURES // P
 
+SECOND_WAY_EVERY = 3
+
 FLOPS = 2 * BATCHES * TOKENS * D_MODEL * 2 * FEATURES + 2 * BATCHES * HEADS * TOKENS * D_HEAD * D_HEAD
 
 assert D_MODEL == K_PASS
@@ -37,12 +40,19 @@ def tile_ufoattention_pa_kernel(tc, queries, Wk, bk, Wv, bv, gamma, out):
         consts = ctx.enter_context(tc.tile_pool(name="consts", bufs=1))
         x_pool = ctx.enter_context(tc.tile_pool(name="x", bufs=GROUPS))
         xt_pool = ctx.enter_context(tc.tile_pool(name="xt", bufs=2))
-        kv_pool = ctx.enter_context(tc.tile_pool(name="kv", bufs=2))
+        kv_pool = ctx.enter_context(tc.tile_pool(name="kv", bufs=4))
+        f32_pool = ctx.enter_context(tc.tile_pool(name="f32", bufs=3))
         kvq_pool = ctx.enter_context(tc.tile_pool(name="kvq", bufs=2 * GROUPS_PER_BATCH))
         end_pool = ctx.enter_context(tc.tile_pool(name="end", bufs=2))
         xt_psum = ctx.enter_context(tc.psum_pool(name="xt_psum", bufs=2))
         proj_psum = ctx.enter_context(tc.psum_pool(name="proj_psum", bufs=5))
         kv_psum = ctx.enter_context(tc.psum_pool(name="kv_psum", bufs=1))
+
+        bias_row = consts.tile([P, 2 * FEATURES], BF16, name="bias_row")
+        nc.vector.memset(bias_row[:], 0.0)
+        ones = consts.tile([P, P], BF16, name="ones")
+        nc.vector.memset(ones[:], 1.0)
+        gamma_all = consts.tile([P, HEADS], BF16, name="gamma_all")
 
         x_groups = queries.flatten_outer_dims().rearrange("(g p j) d -> g p (j d)", p=P, j=PACK)
         x_tiles = []
@@ -52,23 +62,21 @@ def tile_ufoattention_pa_kernel(tc, queries, Wk, bk, Wv, bv, gamma, out):
             nc.sync.dma_start(out=x_sb[:], in_=x_groups[g])
             x_tiles.append(x_sb)
             if g == 0:
-                for w_name, w in (("wk_raw", Wk), ("wv_raw", Wv)):
+                for i, (w_name, w, b_vec) in enumerate((("wk_raw", Wk, bk), ("wv_raw", Wv, bv))):
                     raw = consts.tile([P, PACK, FEATURES], BF16, name=w_name)
                     nc.sync.dma_start(out=raw[:], in_=w.rearrange("(p t) n -> p t n", t=PACK))
                     w_raw.append(raw)
+                    nc.sync.dma_start(
+                        out=bias_row[0:1, i * FEATURES : (i + 1) * FEATURES],
+                        in_=b_vec.rearrange("(o n) -> o n", o=1),
+                    )
+                nc.sync.dma_start(
+                    out=gamma_all[:], in_=gamma.rearrange("a h b c -> (a h b c)").partition_broadcast(P)
+                )
 
         ident = consts.tile([P, P], F32, name="ident")
         make_identity(nc, ident[:])
 
-        bias_row = consts.tile([P, 2 * FEATURES], BF16, name="bias_row")
-        nc.vector.memset(bias_row[:], 0.0)
-        nc.scalar.dma_start(out=bias_row[0:1, 0:FEATURES], in_=bk.rearrange("(o n) -> o n", o=1))
-        nc.scalar.dma_start(out=bias_row[0:1, FEATURES : 2 * FEATURES], in_=bv.rearrange("(o n) -> o n", o=1))
-        ones = consts.tile([P, P], BF16, name="ones")
-        nc.vector.memset(ones[:], 1.0)
-
-        gamma_all = consts.tile([P, HEADS], BF16, name="gamma_all")
-        nc.scalar.dma_start(out=gamma_all[:], in_=gamma.rearrange("a h b c -> (a h b c)").partition_broadcast(P))
         gamma_by_half = gamma_all[:].rearrange("p (pair half) -> p half pair", half=2)
         gain = consts.tile([P, HEAD_PAIRS], F32, name="gain")
         nc.vector.tensor_copy(out=gain[0:D_HEAD, :], in_=gamma_by_half[0:D_HEAD, 0, :])
@@ -118,21 +126,19 @@ def tile_ufoattention_pa_kernel(tc, queries, Wk, bk, Wv, bv, gamma, out):
             nc.tensor.matmul(out=bias_bank[:], lhsT=ones[:], rhs=bias_row[:, cols], start=True, stop=True)
             nc.scalar.copy(out=bias[:, cols], in_=bias_bank[:])
 
-        def finish_batch(b, kv_quantised):
-            kv_bank = kv_psum.tile([P, HEAD_PAIRS, P], F32, name="kv_bank")
-            for pair in range(HEAD_PAIRS):
-                k_cols = slice(pair * P, (pair + 1) * P)
-                v_cols = slice(FEATURES + pair * P, FEATURES + (pair + 1) * P)
-                for c, (codes, scales) in enumerate(kv_quantised):
-                    nc.tensor.matmul_mx(
-                        out=kv_bank[:, pair, :],
-                        lhsT=codes[:, k_cols].bitcast(FP8X4),
-                        lhsT_scale=scales[:, k_cols],
-                        rhs=codes[:, v_cols].bitcast(FP8X4),
-                        rhs_scale=scales[:, v_cols],
-                        start=(c == 0),
-                        stop=(c == GROUPS_PER_BATCH - 1),
-                    )
+        def second_product(kv_bank, pair, kv_quantised):
+            for c, (codes, scales) in enumerate(kv_quantised):
+                nc.tensor.matmul_mx(
+                    out=kv_bank[:, pair, :],
+                    lhsT=codes[:, pair, 0:P].bitcast(FP8X4),
+                    lhsT_scale=scales[:, pair, 0:P],
+                    rhs=codes[:, pair, P : 2 * P].bitcast(FP8X4),
+                    rhs_scale=scales[:, pair, P : 2 * P],
+                    start=(c == 0),
+                    stop=(c == GROUPS_PER_BATCH - 1),
+                )
+
+        def normalise_and_store(b, kv_bank):
             kv = end_pool.tile([P, HEAD_PAIRS, D_HEAD], F32, name="kv")
             for half in range(2):
                 rows = slice(half * D_HEAD, (half + 1) * D_HEAD)
@@ -161,41 +167,55 @@ def tile_ufoattention_pa_kernel(tc, queries, Wk, bk, Wv, bv, gamma, out):
             )
 
         kv_quantised = []
+        banks_done = 0
         for g in range(GROUPS):
             if g + 1 < GROUPS:
                 xt_next = transpose_group(g + 1)
             x_codes, x_scales = x_quantised
-            kv_grouped = kv_pool.tile([P, FEATURE_TILES, P, PACK], BF16, name="kv_grouped", align_bytes=64)
-            for f in range(FEATURE_TILES):
-                f_cols = slice(f * P, (f + 1) * P)
-                proj_bank = proj_psum.tile([P, PACK, P], F32, name="proj_bank")
-                for j in range(PACK):
-                    j_cols = slice(j * P, (j + 1) * P)
-                    nc.tensor.matmul_mx(
-                        out=proj_bank[:, j, :],
-                        lhsT=x_codes[:, j_cols].bitcast(FP8X4),
-                        lhsT_scale=x_scales[:, j_cols],
-                        rhs=w_codes[:, f_cols].bitcast(FP8X4),
-                        rhs_scale=w_scales[:, f_cols],
-                        start=True,
-                        stop=True,
-                    )
-                nc.vector.tensor_tensor(
-                    out=kv_grouped[:, f, :, :],
-                    in0=proj_bank[:].rearrange("p j w -> p w j"),
-                    in1=bias[:, f_cols].unsqueeze(2).to_broadcast([P, P, PACK]),
-                    op=mybir.AluOpType.add,
-                )
-                if f == FEATURE_TILES // 2 - 1 and g + 1 < GROUPS:
-                    x_quantised = quantise_x(xt_next)
-            kv_codes = kvq_pool.tile([P, 2 * FEATURES], U32, name="kv_codes", align_bytes=64)
-            kv_scales = kvq_pool.tile([P, 2 * FEATURES], U8, name="kv_scales", align_bytes=64)
-            nc.vector.quantize_mx(
-                out=kv_codes[:].bitcast(FP8X4),
-                scales=kv_scales[:],
-                in_=kv_grouped[:].rearrange("p f w j -> p (f w j)"),
-            )
+            kv_codes = kvq_pool.tile([P, HEAD_PAIRS, 2 * P], U32, name="kv_codes", align_bytes=64)
+            kv_scales = kvq_pool.tile([P, HEAD_PAIRS, 2 * P], U8, name="kv_scales", align_bytes=64)
             kv_quantised.append((kv_codes, kv_scales))
-            if len(kv_quantised) == GROUPS_PER_BATCH:
-                finish_batch(g // GROUPS_PER_BATCH, kv_quantised)
+            last_of_batch = len(kv_quantised) == GROUPS_PER_BATCH
+            if last_of_batch:
+                kv_bank = kv_psum.tile([P, HEAD_PAIRS, P], F32, name="kv_bank")
+            for pair in range(HEAD_PAIRS):
+                kv_grouped = kv_pool.tile([P, 2, P, PACK], BF16, name="kv_grouped", align_bytes=64)
+                for k_or_v in range(2):
+                    f_cols = slice(k_or_v * FEATURES + pair * P, k_or_v * FEATURES + (pair + 1) * P)
+                    proj_bank = proj_psum.tile([P, PACK, P], F32, name="proj_bank")
+                    for j in range(PACK):
+                        j_cols = slice(j * P, (j + 1) * P)
+                        nc.tensor.matmul_mx(
+                            out=proj_bank[:, j, :],
+                            lhsT=x_codes[:, j_cols].bitcast(FP8X4),
+                            lhsT_scale=x_scales[:, j_cols],
+                            rhs=w_codes[:, f_cols].bitcast(FP8X4),
+                            rhs_scale=w_scales[:, f_cols],
+                            start=True,
+                            stop=True,
+                        )
+                    by_feature = proj_bank[:].rearrange("p j w -> p w j")
+                    bias_by_feature = bias[:, f_cols].unsqueeze(2).to_broadcast([P, P, PACK])
+                    if banks_done % SECOND_WAY_EVERY == 1:
+                        proj_f32 = f32_pool.tile([P, P, PACK], F32, name="proj_f32")
+                        nc.scalar.copy(out=proj_f32[:], in_=by_feature)
+                        nc.gpsimd.tensor_tensor(
+                            out=kv_grouped[:, k_or_v, :, :], in0=proj_f32[:], in1=bias_by_feature, op=ADD
+                        )
+                    else:
+                        nc.vector.tensor_tensor(
+                            out=kv_grouped[:, k_or_v, :, :], in0=by_feature, in1=bias_by_feature, op=ADD
+                        )
+                    banks_done += 1
+                if pair == 1 and g + 1 < GROUPS:
+                    x_quantised = quantise_x(xt_next)
+                nc.vector.quantize_mx(
+                    out=kv_codes[:, pair, :].bitcast(FP8X4),
+                    scales=kv_scales[:, pair, :],
+                    in_=kv_grouped[:].rearrange("p s w j -> p (s w j)"),
+                )
+                if last_of_batch:
+                    second_product(kv_bank, pair, kv_quantised)
+            if last_of_batch:
+                normalise_and_store(g // GROUPS_PER_BATCH, kv_bank)
                 kv_quantised = []

@@ -27,7 +27,7 @@ GROUPS_PER_BATCH = TOKENS // K_PASS
 FEATURE_TILES = 2 * FEATURES // P
 HEAD_PAIRS = FEATURES // P
 
-SECOND_WAY_EVERY = 3
+SECOND_WAY_BANKS = 2
 
 FLOPS = 2 * BATCHES * TOKENS * D_MODEL * 2 * FEATURES + 2 * BATCHES * HEADS * TOKENS * D_HEAD * D_HEAD
 
@@ -40,23 +40,26 @@ def tile_ufoattention_pa_kernel(tc, queries, Wk, bk, Wv, bv, gamma, out):
         consts = ctx.enter_context(tc.tile_pool(name="consts", bufs=1))
         x_pool = ctx.enter_context(tc.tile_pool(name="x", bufs=GROUPS))
         xt_pool = ctx.enter_context(tc.tile_pool(name="xt", bufs=2))
-        kv_pool = ctx.enter_context(tc.tile_pool(name="kv", bufs=4))
-        f32_pool = ctx.enter_context(tc.tile_pool(name="f32", bufs=3))
+        f32_pool = ctx.enter_context(tc.tile_pool(name="f32", bufs=SECOND_WAY_BANKS))
+        kv_pool = ctx.enter_context(tc.tile_pool(name="kv", bufs=1))
         kvq_pool = ctx.enter_context(tc.tile_pool(name="kvq", bufs=2 * GROUPS_PER_BATCH))
         end_pool = ctx.enter_context(tc.tile_pool(name="end", bufs=2))
         xt_psum = ctx.enter_context(tc.psum_pool(name="xt_psum", bufs=2))
         proj_psum = ctx.enter_context(tc.psum_pool(name="proj_psum", bufs=5))
         kv_psum = ctx.enter_context(tc.psum_pool(name="kv_psum", bufs=1))
+        ctx.enter_context(tc.manual_schedule())
 
         bias_row = consts.tile([P, 2 * FEATURES], BF16, name="bias_row")
         nc.vector.memset(bias_row[:], 0.0)
         ones = consts.tile([P, P], BF16, name="ones")
         nc.vector.memset(ones[:], 1.0)
-        gamma_all = consts.tile([P, HEADS], BF16, name="gamma_all")
+        ident = consts.tile([P, P], F32, name="ident")
+        make_identity(nc, ident[:])
 
         x_groups = queries.flatten_outer_dims().rearrange("(g p j) d -> g p (j d)", p=P, j=PACK)
         x_tiles = []
         w_raw = []
+        gamma_all = consts.tile([P, HEADS], BF16, name="gamma_all")
         for g in range(GROUPS):
             x_sb = x_pool.tile([P, PACK * D_MODEL], BF16, name="x_sb")
             nc.sync.dma_start(out=x_sb[:], in_=x_groups[g])
@@ -73,14 +76,6 @@ def tile_ufoattention_pa_kernel(tc, queries, Wk, bk, Wv, bv, gamma, out):
                 nc.sync.dma_start(
                     out=gamma_all[:], in_=gamma.rearrange("a h b c -> (a h b c)").partition_broadcast(P)
                 )
-
-        ident = consts.tile([P, P], F32, name="ident")
-        make_identity(nc, ident[:])
-
-        gamma_by_half = gamma_all[:].rearrange("p (pair half) -> p half pair", half=2)
-        gain = consts.tile([P, HEAD_PAIRS], F32, name="gain")
-        nc.vector.tensor_copy(out=gain[0:D_HEAD, :], in_=gamma_by_half[0:D_HEAD, 0, :])
-        nc.vector.tensor_copy(out=gain[D_HEAD:P, :], in_=gamma_by_half[D_HEAD:P, 1, :])
 
         def transpose_group(g):
             xt_grouped = xt_pool.tile([P, PACK * K_PASS], BF16, name="xt_grouped", align_bytes=64)
@@ -105,19 +100,7 @@ def tile_ufoattention_pa_kernel(tc, queries, Wk, bk, Wv, bv, gamma, out):
             nc.vector.quantize_mx(out=x_codes[:].bitcast(FP8X4), scales=x_scales[:], in_=xt_grouped[:])
             return x_codes, x_scales
 
-        x_quantised = quantise_x(transpose_group(0))
-
-        w_codes = consts.tile([P, 2 * FEATURES], U32, name="w_codes", align_bytes=64)
-        w_scales = consts.tile([P, 2 * FEATURES], U8, name="w_scales", align_bytes=64)
-        for i, w_name in enumerate(("wk_grouped", "wv_grouped")):
-            w_grouped = consts.tile([P, FEATURES, PACK], BF16, name=w_name, align_bytes=64)
-            nc.vector.tensor_copy(out=w_grouped[:], in_=w_raw[i][:].rearrange("p t n -> p n t"))
-            cols = slice(i * FEATURES, (i + 1) * FEATURES)
-            nc.vector.quantize_mx(
-                out=w_codes[:, cols].bitcast(FP8X4),
-                scales=w_scales[:, cols],
-                in_=w_grouped[:].rearrange("p n t -> p (n t)"),
-            )
+        xt_first = transpose_group(0)
 
         bias = consts.tile([P, 2 * FEATURES], F32, name="bias")
         for i in range(2):
@@ -126,19 +109,81 @@ def tile_ufoattention_pa_kernel(tc, queries, Wk, bk, Wv, bv, gamma, out):
             nc.tensor.matmul(out=bias_bank[:], lhsT=ones[:], rhs=bias_row[:, cols], start=True, stop=True)
             nc.scalar.copy(out=bias[:, cols], in_=bias_bank[:])
 
-        def second_product(kv_bank, pair, kv_quantised):
-            for c, (codes, scales) in enumerate(kv_quantised):
-                nc.tensor.matmul_mx(
-                    out=kv_bank[:, pair, :],
-                    lhsT=codes[:, pair, 0:P].bitcast(FP8X4),
-                    lhsT_scale=scales[:, pair, 0:P],
-                    rhs=codes[:, pair, P : 2 * P].bitcast(FP8X4),
-                    rhs_scale=scales[:, pair, P : 2 * P],
-                    start=(c == 0),
-                    stop=(c == GROUPS_PER_BATCH - 1),
-                )
+        w_grouped = []
+        for i, w_name in enumerate(("wk_grouped", "wv_grouped")):
+            grouped = consts.tile([P, FEATURES, PACK], BF16, name=w_name, align_bytes=64)
+            nc.vector.tensor_copy(out=grouped[:], in_=w_raw[i][:].rearrange("p t n -> p n t"))
+            w_grouped.append(grouped)
+        x_quantised = quantise_x(xt_first)
+        w_codes = consts.tile([P, 2 * FEATURES], U32, name="w_codes", align_bytes=64)
+        w_scales = consts.tile([P, 2 * FEATURES], U8, name="w_scales", align_bytes=64)
+        for i in range(2):
+            cols = slice(i * FEATURES, (i + 1) * FEATURES)
+            nc.vector.quantize_mx(
+                out=w_codes[:, cols].bitcast(FP8X4),
+                scales=w_scales[:, cols],
+                in_=w_grouped[i][:].rearrange("p n t -> p (n t)"),
+            )
 
-        def normalise_and_store(b, kv_bank):
+        gamma_by_half = gamma_all[:].rearrange("p (pair half) -> p half pair", half=2)
+        gain = consts.tile([P, HEAD_PAIRS], F32, name="gain")
+        nc.vector.tensor_copy(out=gain[0:D_HEAD, :], in_=gamma_by_half[0:D_HEAD, 0, :])
+        nc.vector.tensor_copy(out=gain[D_HEAD:P, :], in_=gamma_by_half[D_HEAD:P, 1, :])
+
+        def project_group(x_codes, x_scales):
+            kv_grouped = kv_pool.tile([P, FEATURE_TILES, P, PACK], BF16, name="kv_grouped", align_bytes=64)
+            for f in range(FEATURE_TILES):
+                f_cols = slice(f * P, (f + 1) * P)
+                proj_bank = proj_psum.tile([P, PACK, P], F32, name="proj_bank")
+                for j in range(PACK):
+                    j_cols = slice(j * P, (j + 1) * P)
+                    nc.tensor.matmul_mx(
+                        out=proj_bank[:, j, :],
+                        lhsT=x_codes[:, j_cols].bitcast(FP8X4),
+                        lhsT_scale=x_scales[:, j_cols],
+                        rhs=w_codes[:, f_cols].bitcast(FP8X4),
+                        rhs_scale=w_scales[:, f_cols],
+                        start=True,
+                        stop=True,
+                    )
+                by_feature = proj_bank[:].rearrange("p j w -> p w j")
+                bias_by_feature = bias[:, f_cols].unsqueeze(2).to_broadcast([P, P, PACK])
+                if f < SECOND_WAY_BANKS:
+                    proj_f32 = f32_pool.tile([P, P, PACK], F32, name="proj_f32")
+                    nc.scalar.copy(out=proj_f32[:], in_=by_feature)
+                    nc.gpsimd.tensor_tensor(out=kv_grouped[:, f, :, :], in0=proj_f32[:], in1=bias_by_feature, op=ADD)
+                else:
+                    nc.vector.tensor_tensor(out=kv_grouped[:, f, :, :], in0=by_feature, in1=bias_by_feature, op=ADD)
+            return kv_grouped
+
+        def quantise_kv(kv_grouped):
+            kv_codes = kvq_pool.tile([P, 2 * FEATURES], U32, name="kv_codes", align_bytes=64)
+            kv_scales = kvq_pool.tile([P, 2 * FEATURES], U8, name="kv_scales", align_bytes=64)
+            nc.vector.quantize_mx(
+                out=kv_codes[:].bitcast(FP8X4),
+                scales=kv_scales[:],
+                in_=kv_grouped[:].rearrange("p f w j -> p (f w j)"),
+            )
+            return kv_codes, kv_scales
+
+        def second_product(kv_quantised):
+            kv_bank = kv_psum.tile([P, HEAD_PAIRS, P], F32, name="kv_bank")
+            for pair in range(HEAD_PAIRS):
+                k_cols = slice(pair * P, (pair + 1) * P)
+                v_cols = slice(FEATURES + pair * P, FEATURES + (pair + 1) * P)
+                for c, (codes, scales) in enumerate(kv_quantised):
+                    nc.tensor.matmul_mx(
+                        out=kv_bank[:, pair, :],
+                        lhsT=codes[:, k_cols].bitcast(FP8X4),
+                        lhsT_scale=scales[:, k_cols],
+                        rhs=codes[:, v_cols].bitcast(FP8X4),
+                        rhs_scale=scales[:, v_cols],
+                        start=(c == 0),
+                        stop=(c == GROUPS_PER_BATCH - 1),
+                    )
+            return kv_bank
+
+        def row_norms(kv_bank):
             kv = end_pool.tile([P, HEAD_PAIRS, D_HEAD], F32, name="kv")
             for half in range(2):
                 rows = slice(half * D_HEAD, (half + 1) * D_HEAD)
@@ -154,6 +199,9 @@ def tile_ufoattention_pa_kernel(tc, queries, Wk, bk, Wv, bv, gamma, out):
                 )
             norm = end_pool.tile([P, HEAD_PAIRS], F32, name="norm")
             nc.scalar.activation(out=norm[:], in_=sum_squares[:], func=ACT.Sqrt)
+            return kv, norm
+
+        def scale_and_store(b, kv, norm):
             factor = end_pool.tile([P, HEAD_PAIRS], F32, name="factor")
             nc.vector.reciprocal(out=factor[:], in_=norm[:])
             nc.vector.tensor_mul(out=factor[:], in0=factor[:], in1=gain[:])
@@ -167,55 +215,17 @@ def tile_ufoattention_pa_kernel(tc, queries, Wk, bk, Wv, bv, gamma, out):
             )
 
         kv_quantised = []
-        banks_done = 0
-        for g in range(GROUPS):
+        for g in range(GROUPS + 1):
+            batch_ready = g > 0 and g % GROUPS_PER_BATCH == 0
+            if g < GROUPS:
+                kv_grouped = project_group(x_quantised[0], x_quantised[1])
             if g + 1 < GROUPS:
                 xt_next = transpose_group(g + 1)
-            x_codes, x_scales = x_quantised
-            kv_codes = kvq_pool.tile([P, HEAD_PAIRS, 2 * P], U32, name="kv_codes", align_bytes=64)
-            kv_scales = kvq_pool.tile([P, HEAD_PAIRS, 2 * P], U8, name="kv_scales", align_bytes=64)
-            kv_quantised.append((kv_codes, kv_scales))
-            last_of_batch = len(kv_quantised) == GROUPS_PER_BATCH
-            if last_of_batch:
-                kv_bank = kv_psum.tile([P, HEAD_PAIRS, P], F32, name="kv_bank")
-            for pair in range(HEAD_PAIRS):
-                kv_grouped = kv_pool.tile([P, 2, P, PACK], BF16, name="kv_grouped", align_bytes=64)
-                for k_or_v in range(2):
-                    f_cols = slice(k_or_v * FEATURES + pair * P, k_or_v * FEATURES + (pair + 1) * P)
-                    proj_bank = proj_psum.tile([P, PACK, P], F32, name="proj_bank")
-                    for j in range(PACK):
-                        j_cols = slice(j * P, (j + 1) * P)
-                        nc.tensor.matmul_mx(
-                            out=proj_bank[:, j, :],
-                            lhsT=x_codes[:, j_cols].bitcast(FP8X4),
-                            lhsT_scale=x_scales[:, j_cols],
-                            rhs=w_codes[:, f_cols].bitcast(FP8X4),
-                            rhs_scale=w_scales[:, f_cols],
-                            start=True,
-                            stop=True,
-                        )
-                    by_feature = proj_bank[:].rearrange("p j w -> p w j")
-                    bias_by_feature = bias[:, f_cols].unsqueeze(2).to_broadcast([P, P, PACK])
-                    if banks_done % SECOND_WAY_EVERY == 1:
-                        proj_f32 = f32_pool.tile([P, P, PACK], F32, name="proj_f32")
-                        nc.scalar.copy(out=proj_f32[:], in_=by_feature)
-                        nc.gpsimd.tensor_tensor(
-                            out=kv_grouped[:, k_or_v, :, :], in0=proj_f32[:], in1=bias_by_feature, op=ADD
-                        )
-                    else:
-                        nc.vector.tensor_tensor(
-                            out=kv_grouped[:, k_or_v, :, :], in0=by_feature, in1=bias_by_feature, op=ADD
-                        )
-                    banks_done += 1
-                if pair == 1 and g + 1 < GROUPS:
-                    x_quantised = quantise_x(xt_next)
-                nc.vector.quantize_mx(
-                    out=kv_codes[:, pair, :].bitcast(FP8X4),
-                    scales=kv_scales[:, pair, :],
-                    in_=kv_grouped[:].rearrange("p s w j -> p (s w j)"),
-                )
-                if last_of_batch:
-                    second_product(kv_bank, pair, kv_quantised)
-            if last_of_batch:
-                normalise_and_store(g // GROUPS_PER_BATCH, kv_bank)
-                kv_quantised = []
+            if batch_ready:
+                kv, norm = row_norms(second_product(kv_quantised[g - GROUPS_PER_BATCH : g]))
+            if g + 1 < GROUPS:
+                x_quantised = quantise_x(xt_next)
+            if g < GROUPS:
+                kv_quantised.append(quantise_kv(kv_grouped))
+            if batch_ready:
+                scale_and_store(g // GROUPS_PER_BATCH - 1, kv, norm)

@@ -27,7 +27,8 @@ GROUPS_PER_BATCH = TOKENS // K_PASS
 FEATURE_TILES = 2 * FEATURES // P
 HEAD_PAIRS = FEATURES // P
 
-SECOND_WAY_BANKS = 2
+SECOND_WAY_EVERY = 3
+ONES_COLS = 32
 
 FLOPS = 2 * BATCHES * TOKENS * D_MODEL * 2 * FEATURES + 2 * BATCHES * HEADS * TOKENS * D_HEAD * D_HEAD
 
@@ -40,26 +41,24 @@ def tile_ufoattention_pa_kernel(tc, queries, Wk, bk, Wv, bv, gamma, out):
         consts = ctx.enter_context(tc.tile_pool(name="consts", bufs=1))
         x_pool = ctx.enter_context(tc.tile_pool(name="x", bufs=GROUPS))
         xt_pool = ctx.enter_context(tc.tile_pool(name="xt", bufs=2))
-        f32_pool = ctx.enter_context(tc.tile_pool(name="f32", bufs=SECOND_WAY_BANKS))
-        kv_pool = ctx.enter_context(tc.tile_pool(name="kv", bufs=1))
+        kv_pool = ctx.enter_context(tc.tile_pool(name="kv", bufs=4))
+        feat_pool = ctx.enter_context(tc.tile_pool(name="feat", bufs=2))
         kvq_pool = ctx.enter_context(tc.tile_pool(name="kvq", bufs=2 * GROUPS_PER_BATCH))
         end_pool = ctx.enter_context(tc.tile_pool(name="end", bufs=2))
         xt_psum = ctx.enter_context(tc.psum_pool(name="xt_psum", bufs=2))
-        proj_psum = ctx.enter_context(tc.psum_pool(name="proj_psum", bufs=5))
+        proj_psum = ctx.enter_context(tc.psum_pool(name="proj_psum", bufs=4))
+        tok_psum = ctx.enter_context(tc.psum_pool(name="tok_psum", bufs=1))
         kv_psum = ctx.enter_context(tc.psum_pool(name="kv_psum", bufs=1))
-        ctx.enter_context(tc.manual_schedule())
 
         bias_row = consts.tile([P, 2 * FEATURES], BF16, name="bias_row")
         nc.vector.memset(bias_row[:], 0.0)
         ones = consts.tile([P, P], BF16, name="ones")
         nc.vector.memset(ones[:], 1.0)
-        ident = consts.tile([P, P], F32, name="ident")
-        make_identity(nc, ident[:])
+        gamma_all = consts.tile([P, HEADS], BF16, name="gamma_all")
 
         x_groups = queries.flatten_outer_dims().rearrange("(g p j) d -> g p (j d)", p=P, j=PACK)
         x_tiles = []
         w_raw = []
-        gamma_all = consts.tile([P, HEADS], BF16, name="gamma_all")
         for g in range(GROUPS):
             x_sb = x_pool.tile([P, PACK * D_MODEL], BF16, name="x_sb")
             nc.sync.dma_start(out=x_sb[:], in_=x_groups[g])
@@ -76,6 +75,16 @@ def tile_ufoattention_pa_kernel(tc, queries, Wk, bk, Wv, bv, gamma, out):
                 nc.sync.dma_start(
                     out=gamma_all[:], in_=gamma.rearrange("a h b c -> (a h b c)").partition_broadcast(P)
                 )
+
+        ident = consts.tile([P, P], F32, name="ident")
+        make_identity(nc, ident[:])
+        ident_bf16 = consts.tile([P, P], BF16, name="ident_bf16")
+        make_identity(nc, ident_bf16[:])
+
+        gamma_by_half = gamma_all[:].rearrange("p (pair half) -> p half pair", half=2)
+        gain = consts.tile([P, HEAD_PAIRS], F32, name="gain")
+        nc.vector.tensor_copy(out=gain[0:D_HEAD, :], in_=gamma_by_half[0:D_HEAD, 0, :])
+        nc.vector.tensor_copy(out=gain[D_HEAD:P, :], in_=gamma_by_half[D_HEAD:P, 1, :])
 
         def transpose_group(g):
             xt_grouped = xt_pool.tile([P, PACK * K_PASS], BF16, name="xt_grouped", align_bytes=64)
@@ -100,7 +109,22 @@ def tile_ufoattention_pa_kernel(tc, queries, Wk, bk, Wv, bv, gamma, out):
             nc.vector.quantize_mx(out=x_codes[:].bitcast(FP8X4), scales=x_scales[:], in_=xt_grouped[:])
             return x_codes, x_scales
 
-        xt_first = transpose_group(0)
+        x_quantised = quantise_x(transpose_group(0))
+
+        w_codes = consts.tile([P, 2 * FEATURES], U32, name="w_codes", align_bytes=64)
+        w_scales = consts.tile([P, 2 * FEATURES], U8, name="w_scales", align_bytes=64)
+        for i, w_name in enumerate(("wk_grouped", "wv_grouped")):
+            w_grouped = consts.tile([P, FEATURES, PACK], BF16, name=w_name, align_bytes=64)
+            nc.vector.tensor_copy(
+                out=w_grouped[:].rearrange("p (c i) t -> p c t i", i=PACK),
+                in_=w_raw[i][:].rearrange("p t (c i) -> p c t i", i=PACK),
+            )
+            cols = slice(i * FEATURES, (i + 1) * FEATURES)
+            nc.vector.quantize_mx(
+                out=w_codes[:, cols].bitcast(FP8X4),
+                scales=w_scales[:, cols],
+                in_=w_grouped[:].rearrange("p n t -> p (n t)"),
+            )
 
         bias = consts.tile([P, 2 * FEATURES], F32, name="bias")
         for i in range(2):
@@ -108,82 +132,31 @@ def tile_ufoattention_pa_kernel(tc, queries, Wk, bk, Wv, bv, gamma, out):
             bias_bank = proj_psum.tile([P, FEATURES], F32, name="bias_bank", tag="proj_bank")
             nc.tensor.matmul(out=bias_bank[:], lhsT=ones[:], rhs=bias_row[:, cols], start=True, stop=True)
             nc.scalar.copy(out=bias[:, cols], in_=bias_bank[:])
-
-        w_grouped = []
-        for i, w_name in enumerate(("wk_grouped", "wv_grouped")):
-            grouped = consts.tile([P, FEATURES, PACK], BF16, name=w_name, align_bytes=64)
-            nc.vector.tensor_copy(out=grouped[:], in_=w_raw[i][:].rearrange("p t n -> p n t"))
-            w_grouped.append(grouped)
-        x_quantised = quantise_x(xt_first)
-        w_codes = consts.tile([P, 2 * FEATURES], U32, name="w_codes", align_bytes=64)
-        w_scales = consts.tile([P, 2 * FEATURES], U8, name="w_scales", align_bytes=64)
-        for i in range(2):
-            cols = slice(i * FEATURES, (i + 1) * FEATURES)
-            nc.vector.quantize_mx(
-                out=w_codes[:, cols].bitcast(FP8X4),
-                scales=w_scales[:, cols],
-                in_=w_grouped[i][:].rearrange("p n t -> p (n t)"),
+        col_bank = proj_psum.tile([P, FEATURE_TILES, ONES_COLS], F32, name="col_bank", tag="proj_bank")
+        for f in range(FEATURE_TILES):
+            nc.tensor.matmul(
+                out=col_bank[:, f, :],
+                lhsT=bias_row[:, f * P : (f + 1) * P],
+                rhs=ones[:, 0:ONES_COLS],
+                start=True,
+                stop=True,
             )
+        bias_col = consts.tile([P, FEATURE_TILES], F32, name="bias_col")
+        nc.scalar.copy(out=bias_col[:], in_=col_bank[:, :, 0])
 
-        gamma_by_half = gamma_all[:].rearrange("p (pair half) -> p half pair", half=2)
-        gain = consts.tile([P, HEAD_PAIRS], F32, name="gain")
-        nc.vector.tensor_copy(out=gain[0:D_HEAD, :], in_=gamma_by_half[0:D_HEAD, 0, :])
-        nc.vector.tensor_copy(out=gain[D_HEAD:P, :], in_=gamma_by_half[D_HEAD:P, 1, :])
+        def second_product(kv_bank, pair, kv_quantised):
+            for c, (codes, scales) in enumerate(kv_quantised):
+                nc.tensor.matmul_mx(
+                    out=kv_bank[:, pair, :],
+                    lhsT=codes[:, pair, 0:P].bitcast(FP8X4),
+                    lhsT_scale=scales[:, pair, 0:P],
+                    rhs=codes[:, pair, P : 2 * P].bitcast(FP8X4),
+                    rhs_scale=scales[:, pair, P : 2 * P],
+                    start=(c == 0),
+                    stop=(c == GROUPS_PER_BATCH - 1),
+                )
 
-        def project_group(x_codes, x_scales):
-            kv_grouped = kv_pool.tile([P, FEATURE_TILES, P, PACK], BF16, name="kv_grouped", align_bytes=64)
-            for f in range(FEATURE_TILES):
-                f_cols = slice(f * P, (f + 1) * P)
-                proj_bank = proj_psum.tile([P, PACK, P], F32, name="proj_bank")
-                for j in range(PACK):
-                    j_cols = slice(j * P, (j + 1) * P)
-                    nc.tensor.matmul_mx(
-                        out=proj_bank[:, j, :],
-                        lhsT=x_codes[:, j_cols].bitcast(FP8X4),
-                        lhsT_scale=x_scales[:, j_cols],
-                        rhs=w_codes[:, f_cols].bitcast(FP8X4),
-                        rhs_scale=w_scales[:, f_cols],
-                        start=True,
-                        stop=True,
-                    )
-                by_feature = proj_bank[:].rearrange("p j w -> p w j")
-                bias_by_feature = bias[:, f_cols].unsqueeze(2).to_broadcast([P, P, PACK])
-                if f < SECOND_WAY_BANKS:
-                    proj_f32 = f32_pool.tile([P, P, PACK], F32, name="proj_f32")
-                    nc.scalar.copy(out=proj_f32[:], in_=by_feature)
-                    nc.gpsimd.tensor_tensor(out=kv_grouped[:, f, :, :], in0=proj_f32[:], in1=bias_by_feature, op=ADD)
-                else:
-                    nc.vector.tensor_tensor(out=kv_grouped[:, f, :, :], in0=by_feature, in1=bias_by_feature, op=ADD)
-            return kv_grouped
-
-        def quantise_kv(kv_grouped):
-            kv_codes = kvq_pool.tile([P, 2 * FEATURES], U32, name="kv_codes", align_bytes=64)
-            kv_scales = kvq_pool.tile([P, 2 * FEATURES], U8, name="kv_scales", align_bytes=64)
-            nc.vector.quantize_mx(
-                out=kv_codes[:].bitcast(FP8X4),
-                scales=kv_scales[:],
-                in_=kv_grouped[:].rearrange("p f w j -> p (f w j)"),
-            )
-            return kv_codes, kv_scales
-
-        def second_product(kv_quantised):
-            kv_bank = kv_psum.tile([P, HEAD_PAIRS, P], F32, name="kv_bank")
-            for pair in range(HEAD_PAIRS):
-                k_cols = slice(pair * P, (pair + 1) * P)
-                v_cols = slice(FEATURES + pair * P, FEATURES + (pair + 1) * P)
-                for c, (codes, scales) in enumerate(kv_quantised):
-                    nc.tensor.matmul_mx(
-                        out=kv_bank[:, pair, :],
-                        lhsT=codes[:, k_cols].bitcast(FP8X4),
-                        lhsT_scale=scales[:, k_cols],
-                        rhs=codes[:, v_cols].bitcast(FP8X4),
-                        rhs_scale=scales[:, v_cols],
-                        start=(c == 0),
-                        stop=(c == GROUPS_PER_BATCH - 1),
-                    )
-            return kv_bank
-
-        def row_norms(kv_bank):
+        def normalise_and_store(b, kv_bank):
             kv = end_pool.tile([P, HEAD_PAIRS, D_HEAD], F32, name="kv")
             for half in range(2):
                 rows = slice(half * D_HEAD, (half + 1) * D_HEAD)
@@ -199,9 +172,6 @@ def tile_ufoattention_pa_kernel(tc, queries, Wk, bk, Wv, bv, gamma, out):
                 )
             norm = end_pool.tile([P, HEAD_PAIRS], F32, name="norm")
             nc.scalar.activation(out=norm[:], in_=sum_squares[:], func=ACT.Sqrt)
-            return kv, norm
-
-        def scale_and_store(b, kv, norm):
             factor = end_pool.tile([P, HEAD_PAIRS], F32, name="factor")
             nc.vector.reciprocal(out=factor[:], in_=norm[:])
             nc.vector.tensor_mul(out=factor[:], in0=factor[:], in1=gain[:])
@@ -215,17 +185,72 @@ def tile_ufoattention_pa_kernel(tc, queries, Wk, bk, Wv, bv, gamma, out):
             )
 
         kv_quantised = []
-        for g in range(GROUPS + 1):
-            batch_ready = g > 0 and g % GROUPS_PER_BATCH == 0
-            if g < GROUPS:
-                kv_grouped = project_group(x_quantised[0], x_quantised[1])
+        banks_done = 0
+        for g in range(GROUPS):
             if g + 1 < GROUPS:
                 xt_next = transpose_group(g + 1)
-            if batch_ready:
-                kv, norm = row_norms(second_product(kv_quantised[g - GROUPS_PER_BATCH : g]))
-            if g + 1 < GROUPS:
-                x_quantised = quantise_x(xt_next)
-            if g < GROUPS:
-                kv_quantised.append(quantise_kv(kv_grouped))
-            if batch_ready:
-                scale_and_store(g // GROUPS_PER_BATCH - 1, kv, norm)
+            x_codes, x_scales = x_quantised
+            kv_codes = kvq_pool.tile([P, HEAD_PAIRS, 2 * P], U32, name="kv_codes", align_bytes=64)
+            kv_scales = kvq_pool.tile([P, HEAD_PAIRS, 2 * P], U8, name="kv_scales", align_bytes=64)
+            kv_quantised.append((kv_codes, kv_scales))
+            last_of_batch = len(kv_quantised) == GROUPS_PER_BATCH
+            if last_of_batch:
+                kv_bank = kv_psum.tile([P, HEAD_PAIRS, P], F32, name="kv_bank")
+            for pair in range(HEAD_PAIRS):
+                kv_grouped = kv_pool.tile([P, 2, P, PACK], BF16, name="kv_grouped", align_bytes=64)
+                for k_or_v in range(2):
+                    f = k_or_v * HEAD_PAIRS + pair
+                    f_cols = slice(f * P, (f + 1) * P)
+                    if banks_done % SECOND_WAY_EVERY == 1:
+                        feat_bank = proj_psum.tile([P, K_PASS], F32, name="feat_bank", tag="proj_bank")
+                        nc.tensor.matmul_mx(
+                            out=feat_bank[:],
+                            lhsT=w_codes[:, f_cols].bitcast(FP8X4),
+                            lhsT_scale=w_scales[:, f_cols],
+                            rhs=x_codes[:].bitcast(FP8X4),
+                            rhs_scale=x_scales[:],
+                            start=True,
+                            stop=True,
+                        )
+                        feat_sb = feat_pool.tile([P, K_PASS], BF16, name="feat_sb")
+                        nc.scalar.activation(
+                            out=feat_sb[:], in_=feat_bank[:], func=ACT.Identity, bias=bias_col[:, f : f + 1]
+                        )
+                        tok_bank = tok_psum.tile([P, PACK, P], BF16, name="tok_bank")
+                        for j in range(PACK):
+                            nc.tensor.transpose(tok_bank[:, j, :], feat_sb[:, j * P : (j + 1) * P], ident_bf16[:])
+                        nc.scalar.copy(
+                            out=kv_grouped[:, k_or_v, :, :], in_=tok_bank[:].rearrange("p j w -> p w j")
+                        )
+                    else:
+                        proj_bank = proj_psum.tile([P, PACK, P], F32, name="proj_bank")
+                        for j in range(PACK):
+                            j_cols = slice(j * P, (j + 1) * P)
+                            nc.tensor.matmul_mx(
+                                out=proj_bank[:, j, :],
+                                lhsT=x_codes[:, j_cols].bitcast(FP8X4),
+                                lhsT_scale=x_scales[:, j_cols],
+                                rhs=w_codes[:, f_cols].bitcast(FP8X4),
+                                rhs_scale=w_scales[:, f_cols],
+                                start=True,
+                                stop=True,
+                            )
+                        nc.vector.tensor_tensor(
+                            out=kv_grouped[:, k_or_v, :, :],
+                            in0=proj_bank[:].rearrange("p j w -> p w j"),
+                            in1=bias[:, f_cols].unsqueeze(2).to_broadcast([P, P, PACK]),
+                            op=ADD,
+                        )
+                    banks_done += 1
+                if pair == 1 and g + 1 < GROUPS:
+                    x_quantised = quantise_x(xt_next)
+                nc.vector.quantize_mx(
+                    out=kv_codes[:, pair, :].bitcast(FP8X4),
+                    scales=kv_scales[:, pair, :],
+                    in_=kv_grouped[:].rearrange("p s w j -> p (s w j)"),
+                )
+                if last_of_batch:
+                    second_product(kv_bank, pair, kv_quantised)
+            if last_of_batch:
+                normalise_and_store(g // GROUPS_PER_BATCH, kv_bank)
+                kv_quantised = []

@@ -9,7 +9,8 @@ U32 = mybir.dt.uint32
 U8 = mybir.dt.uint8
 FP8X4 = mybir.dt.float8_e4m3fn_x4
 ACT = mybir.ActivationFunctionType
-ADD = mybir.AluOpType.add
+ALU = mybir.AluOpType
+AX = mybir.AxisListType
 
 P = 128
 PACK = 4
@@ -23,16 +24,14 @@ D_HEAD = 64
 FEATURES = HEADS * D_HEAD
 
 GROUPS = BATCHES * TOKENS // K_PASS
-GROUPS_PER_BATCH = TOKENS // K_PASS
-FEATURE_TILES = 2 * FEATURES // P
 HEAD_PAIRS = FEATURES // P
-
-SECOND_WAY_EVERY = 3
+WAY_PAIRS = HEAD_PAIRS // 2
+HALF = FEATURES // 2
 ONES_COLS = 32
 
 FLOPS = 2 * BATCHES * TOKENS * D_MODEL * 2 * FEATURES + 2 * BATCHES * HEADS * TOKENS * D_HEAD * D_HEAD
 
-assert D_MODEL == K_PASS
+TILES = [(0, 0), (1, 0), (0, 1), (1, 1)]
 
 
 def tile_ufoattention_pa_kernel(tc, queries, Wk, bk, Wv, bv, gamma, out):
@@ -40,21 +39,30 @@ def tile_ufoattention_pa_kernel(tc, queries, Wk, bk, Wv, bv, gamma, out):
     with ExitStack() as ctx:
         consts = ctx.enter_context(tc.tile_pool(name="consts", bufs=1))
         x_pool = ctx.enter_context(tc.tile_pool(name="x", bufs=GROUPS))
-        xt_pool = ctx.enter_context(tc.tile_pool(name="xt", bufs=2))
-        kv_pool = ctx.enter_context(tc.tile_pool(name="kv", bufs=4))
-        feat_pool = ctx.enter_context(tc.tile_pool(name="feat", bufs=2))
-        kvq_pool = ctx.enter_context(tc.tile_pool(name="kvq", bufs=2 * GROUPS_PER_BATCH))
+        xt_pool = ctx.enter_context(tc.tile_pool(name="xt", bufs=3))
+        kv_pool = ctx.enter_context(tc.tile_pool(name="kv", bufs=2))
+        feat_pool = ctx.enter_context(tc.tile_pool(name="feat", bufs=8))
+        kvq_pool = ctx.enter_context(tc.tile_pool(name="kvq", bufs=4))
         end_pool = ctx.enter_context(tc.tile_pool(name="end", bufs=2))
-        xt_psum = ctx.enter_context(tc.psum_pool(name="xt_psum", bufs=2))
-        proj_psum = ctx.enter_context(tc.psum_pool(name="proj_psum", bufs=4))
-        tok_psum = ctx.enter_context(tc.psum_pool(name="tok_psum", bufs=1))
-        kv_psum = ctx.enter_context(tc.psum_pool(name="kv_psum", bufs=1))
+        tr_psum = ctx.enter_context(tc.psum_pool(name="tr_psum", bufs=3))
+        feat_psum = ctx.enter_context(tc.psum_pool(name="feat_psum", bufs=2))
+        proj_psum = ctx.enter_context(tc.psum_pool(name="proj_psum", bufs=3))
+        ctx.enter_context(tc.manual_schedule())
 
+        warm = consts.tile([P, 1], F32, name="warm")
+        nc.vector.memset(warm[:], 1.0)
         bias_row = consts.tile([P, 2 * FEATURES], BF16, name="bias_row")
         nc.vector.memset(bias_row[:], 0.0)
         ones = consts.tile([P, P], BF16, name="ones")
         nc.vector.memset(ones[:], 1.0)
-        gamma_all = consts.tile([P, HEADS], BF16, name="gamma_all")
+        ident = consts.tile([P, P], F32, name="ident")
+        make_identity(nc, ident[:])
+        nc.scalar.activation(out=warm[:], in_=warm[:], func=ACT.Sqrt)
+        for i, b_vec in enumerate((bk, bv)):
+            nc.scalar.dma_start(
+                out=bias_row[0:1, i * FEATURES : (i + 1) * FEATURES],
+                in_=b_vec.rearrange("(o n) -> o n", o=1),
+            )
 
         x_groups = queries.flatten_outer_dims().rearrange("(g p j) d -> g p (j d)", p=P, j=PACK)
         x_tiles = []
@@ -64,43 +72,29 @@ def tile_ufoattention_pa_kernel(tc, queries, Wk, bk, Wv, bv, gamma, out):
             nc.sync.dma_start(out=x_sb[:], in_=x_groups[g])
             x_tiles.append(x_sb)
             if g == 0:
-                for i, (w_name, w, b_vec) in enumerate((("wk_raw", Wk, bk), ("wv_raw", Wv, bv))):
-                    raw = consts.tile([P, PACK, FEATURES], BF16, name=w_name)
-                    nc.sync.dma_start(out=raw[:], in_=w.rearrange("(p t) n -> p t n", t=PACK))
+                for w_name, w in (("wk_raw", Wk), ("wv_raw", Wv)):
+                    raw = consts.tile([P, 2, 2, FEATURES], BF16, name=w_name)
+                    nc.sync.dma_start(out=raw[:], in_=w.rearrange("(s q e) n -> q s e n", s=2, e=2))
                     w_raw.append(raw)
-                    nc.sync.dma_start(
-                        out=bias_row[0:1, i * FEATURES : (i + 1) * FEATURES],
-                        in_=b_vec.rearrange("(o n) -> o n", o=1),
-                    )
-                nc.sync.dma_start(
-                    out=gamma_all[:], in_=gamma.rearrange("a h b c -> (a h b c)").partition_broadcast(P)
-                )
-
-        ident = consts.tile([P, P], F32, name="ident")
-        make_identity(nc, ident[:])
-        ident_bf16 = consts.tile([P, P], BF16, name="ident_bf16")
-        make_identity(nc, ident_bf16[:])
-
-        gamma_by_half = gamma_all[:].rearrange("p (pair half) -> p half pair", half=2)
-        gain = consts.tile([P, HEAD_PAIRS], F32, name="gain")
-        nc.vector.tensor_copy(out=gain[0:D_HEAD, :], in_=gamma_by_half[0:D_HEAD, 0, :])
-        nc.vector.tensor_copy(out=gain[D_HEAD:P, :], in_=gamma_by_half[D_HEAD:P, 1, :])
+        gamma_all = consts.tile([P, HEADS], BF16, name="gamma_all")
+        nc.sync.dma_start(out=gamma_all[:], in_=gamma.rearrange("a h b c -> (a h b c)").partition_broadcast(P))
 
         def transpose_group(g):
+            x_words = x_tiles[g][:].bitcast(F32).rearrange("p (j s q) -> p j s q", j=PACK, s=2)
+            banks = []
+            for u in range(2):
+                bank = tr_psum.tile([P, PACK, P], F32, name="xt_bank", tag="tr_bank")
+                for e in range(2):
+                    for s in range(2):
+                        nc.tensor.transpose(bank[:, 2 * e + s, :], x_words[:, 2 * u + e, s, :], ident[:])
+                banks.append(bank)
+            return banks
+
+        def copy_group(banks):
             xt_grouped = xt_pool.tile([P, PACK * K_PASS], BF16, name="xt_grouped", align_bytes=64)
-            x_words = x_tiles[g][:].bitcast(F32).rearrange("p (j q u) -> p j u q", j=PACK, u=2)
-            grouped_words = xt_grouped[:].bitcast(F32).rearrange("q (m u) -> q m u", u=2)
-            for half in range(2):
-                xt_bank = xt_psum.tile([P, 2, 2 * P], F32, name="xt_bank")
-                for jj in range(2):
-                    for u in range(2):
-                        nc.tensor.transpose(
-                            xt_bank[:, u, jj * P : (jj + 1) * P], x_words[:, 2 * half + jj, u, :], ident[:]
-                        )
-                nc.scalar.copy(
-                    out=grouped_words[:, half * 2 * P : (half + 1) * 2 * P, :],
-                    in_=xt_bank[:].rearrange("q u m -> q m u"),
-                )
+            words = xt_grouped[:].bitcast(F32).rearrange("q (u p f) -> q u p f", u=2, f=PACK)
+            for u in range(2):
+                nc.scalar.copy(out=words[:, u, :, :], in_=banks[u][:].rearrange("q f p -> q p f"))
             return xt_grouped
 
         def quantise_x(xt_grouped):
@@ -109,148 +103,220 @@ def tile_ufoattention_pa_kernel(tc, queries, Wk, bk, Wv, bv, gamma, out):
             nc.vector.quantize_mx(out=x_codes[:].bitcast(FP8X4), scales=x_scales[:], in_=xt_grouped[:])
             return x_codes, x_scales
 
-        x_quantised = quantise_x(transpose_group(0))
+        xq = {}
+        xt0 = copy_group(transpose_group(0))
 
-        w_codes = consts.tile([P, 2 * FEATURES], U32, name="w_codes", align_bytes=64)
-        w_scales = consts.tile([P, 2 * FEATURES], U8, name="w_scales", align_bytes=64)
+        w_codes = consts.tile([P, 2, FEATURES], U32, name="w_codes", align_bytes=64)
+        w_scales = consts.tile([P, 2, FEATURES], U8, name="w_scales", align_bytes=64)
+        w_grouped = []
         for i, w_name in enumerate(("wk_grouped", "wv_grouped")):
-            w_grouped = consts.tile([P, FEATURES, PACK], BF16, name=w_name, align_bytes=64)
-            nc.vector.tensor_copy(
-                out=w_grouped[:].rearrange("p (c i) t -> p c t i", i=PACK),
-                in_=w_raw[i][:].rearrange("p t (c i) -> p c t i", i=PACK),
-            )
-            cols = slice(i * FEATURES, (i + 1) * FEATURES)
-            nc.vector.quantize_mx(
-                out=w_codes[:, cols].bitcast(FP8X4),
-                scales=w_scales[:, cols],
-                in_=w_grouped[:].rearrange("p n t -> p (n t)"),
+            w_grouped.append(consts.tile([P, FEATURES, PACK], BF16, name=w_name, align_bytes=64))
+
+        def regroup_w(copy, i, lo, hi):
+            copy(
+                out=w_grouped[i][:, lo:hi, :].rearrange("p (c i) t -> p c t i", i=PACK),
+                in_=w_raw[i][:].rearrange("p s e n -> p (s e) n")[:, :, lo:hi].rearrange("p t (c i) -> p c t i", i=PACK),
             )
 
-        bias = consts.tile([P, 2 * FEATURES], F32, name="bias")
+        def quantise_w(i):
+            nc.vector.quantize_mx(
+                out=w_codes[:, i, :].bitcast(FP8X4),
+                scales=w_scales[:, i, :],
+                in_=w_grouped[i][:].rearrange("p n t -> p (n t)"),
+            )
+
+        regroup_w(nc.vector.tensor_copy, 0, 0, FEATURES)
+        xq[0] = quantise_x(xt0)
+        quantise_w(0)
+        regroup_w(nc.scalar.copy, 1, HALF, FEATURES)
+        regroup_w(nc.vector.tensor_copy, 1, 0, HALF)
+
+        bias_bank = proj_psum.tile([P, 2, HALF], F32, name="bias_bank", tag="proj_bank")
         for i in range(2):
-            cols = slice(i * FEATURES, (i + 1) * FEATURES)
-            bias_bank = proj_psum.tile([P, FEATURES], F32, name="bias_bank", tag="proj_bank")
-            nc.tensor.matmul(out=bias_bank[:], lhsT=ones[:], rhs=bias_row[:, cols], start=True, stop=True)
-            nc.scalar.copy(out=bias[:, cols], in_=bias_bank[:])
-        col_bank = proj_psum.tile([P, FEATURE_TILES, ONES_COLS], F32, name="col_bank", tag="proj_bank")
-        for f in range(FEATURE_TILES):
             nc.tensor.matmul(
-                out=col_bank[:, f, :],
-                lhsT=bias_row[:, f * P : (f + 1) * P],
-                rhs=ones[:, 0:ONES_COLS],
+                out=bias_bank[:, i, :],
+                lhsT=ones[:],
+                rhs=bias_row[:, i * FEATURES : i * FEATURES + HALF],
                 start=True,
                 stop=True,
             )
-        bias_col = consts.tile([P, FEATURE_TILES], F32, name="bias_col")
+        col_bank = proj_psum.tile([P, PACK, ONES_COLS], F32, name="col_bank", tag="proj_bank")
+        for n, (pair, i) in enumerate(TILES):
+            lo = i * FEATURES + HALF + pair * P
+            nc.tensor.matmul(
+                out=col_bank[:, n, :], lhsT=bias_row[:, lo : lo + P], rhs=ones[:, 0:ONES_COLS], start=True, stop=True
+            )
+        bias = consts.tile([P, 2, HALF], F32, name="bias")
+        nc.scalar.copy(out=bias[:], in_=bias_bank[:])
+        bias_col = consts.tile([P, PACK], F32, name="bias_col")
         nc.scalar.copy(out=bias_col[:], in_=col_bank[:, :, 0])
 
-        def second_product(kv_bank, pair, kv_quantised):
-            for c, (codes, scales) in enumerate(kv_quantised):
-                nc.tensor.matmul_mx(
-                    out=kv_bank[:, pair, :],
-                    lhsT=codes[:, pair, 0:P].bitcast(FP8X4),
-                    lhsT_scale=scales[:, pair, 0:P],
-                    rhs=codes[:, pair, P : 2 * P].bitcast(FP8X4),
-                    rhs_scale=scales[:, pair, P : 2 * P],
-                    start=(c == 0),
-                    stop=(c == GROUPS_PER_BATCH - 1),
-                )
+        xt1 = copy_group(transpose_group(1))
+        quantise_w(1)
+        xq[1] = quantise_x(xt1)
 
-        def normalise_and_store(b, kv_bank):
-            kv = end_pool.tile([P, HEAD_PAIRS, D_HEAD], F32, name="kv")
-            for half in range(2):
-                rows = slice(half * D_HEAD, (half + 1) * D_HEAD)
-                nc.scalar.copy(out=kv[rows, :, :], in_=kv_bank[rows, :, half * D_HEAD : (half + 1) * D_HEAD])
-            squares = end_pool.tile([P, HEAD_PAIRS, D_HEAD], F32, name="squares")
-            sum_squares = end_pool.tile([P, HEAD_PAIRS], F32, name="sum_squares")
-            for pair in range(HEAD_PAIRS):
-                nc.scalar.activation(
-                    out=squares[:, pair, :],
-                    in_=kv[:, pair, :],
-                    func=ACT.Square,
-                    accum_out=sum_squares[:, pair : pair + 1],
+        grouped1 = {}
+        grouped2 = {}
+        codes1 = {}
+        codes2 = {}
+        feats = {}
+
+        def way2_tile(g, n):
+            pair, i = TILES[n]
+            lo = HALF + pair * P
+            x_codes, x_scales = xq[g]
+            bank = feat_psum.tile([P, K_PASS], F32, name="feat_bank")
+            nc.tensor.matmul_mx(
+                out=bank[:],
+                lhsT=w_codes[:, i, lo : lo + P].bitcast(FP8X4),
+                lhsT_scale=w_scales[:, i, lo : lo + P],
+                rhs=x_codes[:].bitcast(FP8X4),
+                rhs_scale=x_scales[:],
+                start=True,
+                stop=True,
+            )
+            feat_sb = feat_pool.tile([P, K_PASS], BF16, name="feat_sb")
+            nc.scalar.activation(out=feat_sb[:], in_=bank[:], func=ACT.Identity, bias=bias_col[:, n : n + 1])
+            feats[g, pair, i] = feat_sb
+
+        def way1_tile(g, n):
+            pair, i = TILES[n]
+            lo = pair * P
+            x_codes, x_scales = xq[g]
+            bank = proj_psum.tile([P, PACK, P], F32, name="proj_bank", tag="proj_bank")
+            for j in range(PACK):
+                cols = slice(j * P, (j + 1) * P)
+                nc.tensor.matmul_mx(
+                    out=bank[:, j, :],
+                    lhsT=x_codes[:, cols].bitcast(FP8X4),
+                    lhsT_scale=x_scales[:, cols],
+                    rhs=w_codes[:, i, lo : lo + P].bitcast(FP8X4),
+                    rhs_scale=w_scales[:, i, lo : lo + P],
+                    start=True,
+                    stop=True,
                 )
-            norm = end_pool.tile([P, HEAD_PAIRS], F32, name="norm")
-            nc.scalar.activation(out=norm[:], in_=sum_squares[:], func=ACT.Sqrt)
-            factor = end_pool.tile([P, HEAD_PAIRS], F32, name="factor")
-            nc.vector.reciprocal(out=factor[:], in_=norm[:])
-            nc.vector.tensor_mul(out=factor[:], in0=factor[:], in1=gain[:])
-            result = end_pool.tile([P, HEAD_PAIRS, D_HEAD], F32, name="result")
-            for pair in range(HEAD_PAIRS):
-                nc.scalar.activation(
-                    out=result[:, pair, :], in_=kv[:, pair, :], func=ACT.Copy, scale=factor[:, pair : pair + 1]
-                )
-            nc.sync.dma_start(
-                out=out[b].rearrange("(pair half) i j -> (half i) pair j", half=2), in_=result[:]
+            nc.vector.tensor_tensor(
+                out=grouped1[g][:, pair, i, :, :],
+                in0=bank[:].rearrange("p j w -> p w j"),
+                in1=bias[:, i, lo : lo + P].unsqueeze(2).to_broadcast([P, P, PACK]),
+                op=ALU.add,
             )
 
-        kv_quantised = []
-        banks_done = 0
+        def transpose_back(g):
+            banks = []
+            for pair in range(WAY_PAIRS):
+                bank = tr_psum.tile([P, 2, 2, P], F32, name="tok_bank", tag="tr_bank")
+                for i in range(2):
+                    words = feats[g, pair, i][:].bitcast(F32)
+                    for u in range(2):
+                        nc.tensor.transpose(bank[:, i, u, :], words[:, u * P : (u + 1) * P], ident[:])
+                banks.append(bank)
+            return banks
+
+        def copy_back(g, banks):
+            for pair in range(WAY_PAIRS):
+                words = grouped2[g][:].rearrange("p a i f t -> p (a i f t)").bitcast(F32)
+                words = words.rearrange("p (a i f u) -> p a i f u", a=WAY_PAIRS, i=2, u=2)
+                nc.scalar.copy(out=words[:, pair, :, :, :], in_=banks[pair][:].rearrange("p i u f -> p i f u"))
+
+        def quantise_kv(grouped, name):
+            codes = kvq_pool.tile([P, WAY_PAIRS, 2, P], U32, name=name + "_codes", align_bytes=64)
+            scales = kvq_pool.tile([P, WAY_PAIRS, 2, P], U8, name=name + "_scales", align_bytes=64)
+            nc.vector.quantize_mx(
+                out=codes[:].rearrange("p a i f -> p (a i f)").bitcast(FP8X4),
+                scales=scales[:].rearrange("p a i f -> p (a i f)"),
+                in_=grouped[:].rearrange("p a i f t -> p (a i f t)"),
+            )
+            return codes, scales
+
+        def second_product(b, kv_bank, half):
+            store = (codes1, codes2)[half]
+            for pair in range(WAY_PAIRS):
+                for c in range(2):
+                    codes, scales = store[2 * b + c]
+                    nc.tensor.matmul_mx(
+                        out=kv_bank[:, 2 * half + pair, :],
+                        lhsT=codes[:, pair, 0, :].bitcast(FP8X4),
+                        lhsT_scale=scales[:, pair, 0, :],
+                        rhs=codes[:, pair, 1, :].bitcast(FP8X4),
+                        rhs_scale=scales[:, pair, 1, :],
+                        start=(c == 0),
+                        stop=(c == 1),
+                    )
+
+        gain = consts.tile([P, HEAD_PAIRS], F32, name="gain")
+
+        def load_gain():
+            gamma_by_half = gamma_all[:].rearrange("p (pair half) -> p half pair", half=2)
+            nc.gpsimd.tensor_copy(out=gain[0:D_HEAD, :], in_=gamma_by_half[0:D_HEAD, 0, :])
+            nc.gpsimd.tensor_copy(out=gain[D_HEAD:P, :], in_=gamma_by_half[D_HEAD:P, 1, :])
+
+        ends = {}
+
+        def end_copy(kv_bank):
+            kv = end_pool.tile([P, HEAD_PAIRS, D_HEAD], F32, name="kv")
+            nc.scalar.copy(out=kv[0:D_HEAD, :, :], in_=kv_bank[0:D_HEAD, :, 0:D_HEAD])
+            nc.vector.tensor_copy(out=kv[D_HEAD:P, :, :], in_=kv_bank[D_HEAD:P, :, D_HEAD:P])
+            squares = end_pool.tile([P, HEAD_PAIRS, D_HEAD], F32, name="squares")
+            nc.gpsimd.tensor_tensor(out=squares[:], in0=kv[:], in1=kv[:], op=ALU.mult)
+            return kv, squares
+
+        def end_norm(squares):
+            total = end_pool.tile([P, HEAD_PAIRS], F32, name="total")
+            nc.vector.tensor_reduce(out=total[:], in_=squares[:], axis=AX.X, op=ALU.add)
+            norm = end_pool.tile([P, HEAD_PAIRS], F32, name="norm")
+            nc.scalar.activation(out=norm[:], in_=total[:], func=ACT.Sqrt)
+            return norm
+
+        def end_store(b, kv, norm):
+            factor = end_pool.tile([P, HEAD_PAIRS], F32, name="factor")
+            nc.vector.reciprocal(out=factor[:], in_=norm[:])
+            nc.gpsimd.tensor_tensor(out=factor[:], in0=factor[:], in1=gain[:], op=ALU.mult)
+            result = end_pool.tile([P, HEAD_PAIRS, D_HEAD], F32, name="result")
+            nc.gpsimd.tensor_tensor(
+                out=result[:],
+                in0=kv[:],
+                in1=factor[:].unsqueeze(2).to_broadcast([P, HEAD_PAIRS, D_HEAD]),
+                op=ALU.mult,
+            )
+            nc.sync.dma_start(out=out[b].rearrange("(pair half) i j -> (half i) pair j", half=2), in_=result[:])
+
+        kv_banks = {}
         for g in range(GROUPS):
-            if g + 1 < GROUPS:
-                xt_next = transpose_group(g + 1)
-            x_codes, x_scales = x_quantised
-            kv_codes = kvq_pool.tile([P, HEAD_PAIRS, 2 * P], U32, name="kv_codes", align_bytes=64)
-            kv_scales = kvq_pool.tile([P, HEAD_PAIRS, 2 * P], U8, name="kv_scales", align_bytes=64)
-            kv_quantised.append((kv_codes, kv_scales))
-            last_of_batch = len(kv_quantised) == GROUPS_PER_BATCH
-            if last_of_batch:
-                kv_bank = kv_psum.tile([P, HEAD_PAIRS, P], F32, name="kv_bank")
-            for pair in range(HEAD_PAIRS):
-                kv_grouped = kv_pool.tile([P, 2, P, PACK], BF16, name="kv_grouped", align_bytes=64)
-                for k_or_v in range(2):
-                    f = k_or_v * HEAD_PAIRS + pair
-                    f_cols = slice(f * P, (f + 1) * P)
-                    if banks_done % SECOND_WAY_EVERY == 1:
-                        feat_bank = proj_psum.tile([P, K_PASS], F32, name="feat_bank", tag="proj_bank")
-                        nc.tensor.matmul_mx(
-                            out=feat_bank[:],
-                            lhsT=w_codes[:, f_cols].bitcast(FP8X4),
-                            lhsT_scale=w_scales[:, f_cols],
-                            rhs=x_codes[:].bitcast(FP8X4),
-                            rhs_scale=x_scales[:],
-                            start=True,
-                            stop=True,
-                        )
-                        feat_sb = feat_pool.tile([P, K_PASS], BF16, name="feat_sb")
-                        nc.scalar.activation(
-                            out=feat_sb[:], in_=feat_bank[:], func=ACT.Identity, bias=bias_col[:, f : f + 1]
-                        )
-                        tok_bank = tok_psum.tile([P, PACK, P], BF16, name="tok_bank")
-                        for j in range(PACK):
-                            nc.tensor.transpose(tok_bank[:, j, :], feat_sb[:, j * P : (j + 1) * P], ident_bf16[:])
-                        nc.scalar.copy(
-                            out=kv_grouped[:, k_or_v, :, :], in_=tok_bank[:].rearrange("p j w -> p w j")
-                        )
-                    else:
-                        proj_bank = proj_psum.tile([P, PACK, P], F32, name="proj_bank")
-                        for j in range(PACK):
-                            j_cols = slice(j * P, (j + 1) * P)
-                            nc.tensor.matmul_mx(
-                                out=proj_bank[:, j, :],
-                                lhsT=x_codes[:, j_cols].bitcast(FP8X4),
-                                lhsT_scale=x_scales[:, j_cols],
-                                rhs=w_codes[:, f_cols].bitcast(FP8X4),
-                                rhs_scale=w_scales[:, f_cols],
-                                start=True,
-                                stop=True,
-                            )
-                        nc.vector.tensor_tensor(
-                            out=kv_grouped[:, k_or_v, :, :],
-                            in0=proj_bank[:].rearrange("p j w -> p w j"),
-                            in1=bias[:, f_cols].unsqueeze(2).to_broadcast([P, P, PACK]),
-                            op=ADD,
-                        )
-                    banks_done += 1
-                if pair == 1 and g + 1 < GROUPS:
-                    x_quantised = quantise_x(xt_next)
-                nc.vector.quantize_mx(
-                    out=kv_codes[:, pair, :].bitcast(FP8X4),
-                    scales=kv_scales[:, pair, :],
-                    in_=kv_grouped[:].rearrange("p s w j -> p (s w j)"),
-                )
-                if last_of_batch:
-                    second_product(kv_bank, pair, kv_quantised)
-            if last_of_batch:
-                normalise_and_store(g // GROUPS_PER_BATCH, kv_bank)
-                kv_quantised = []
+            ending = g // 2 - 1 if g % 2 == 1 and g > 1 else None
+            grouped1[g] = kv_pool.tile([P, WAY_PAIRS, 2, P, PACK], BF16, name="kv_grouped1", align_bytes=64)
+            grouped2[g] = kv_pool.tile([P, WAY_PAIRS, 2, P, PACK], BF16, name="kv_grouped2", align_bytes=64)
+            for n in range(4):
+                way2_tile(g, n)
+                way1_tile(g, n)
+                if ending is not None:
+                    if n == 0:
+                        if ending == 0:
+                            load_gain()
+                        kv, squares = end_copy(kv_banks[ending])
+                    elif n == 2:
+                        norm = end_norm(squares)
+                    elif n == 3:
+                        end_store(ending, kv, norm)
+            if g + 2 < GROUPS:
+                xt = copy_group(transpose_group(g + 2))
+            if g > 0:
+                codes2[g - 1] = quantise_kv(grouped2[g - 1], "kv2")
+            codes1[g] = quantise_kv(grouped1[g], "kv1")
+            copy_back(g, transpose_back(g))
+            if g + 2 < GROUPS:
+                xq[g + 2] = quantise_x(xt)
+            if g % 2 == 0 and g > 0:
+                b = g // 2 - 1
+                kv_banks[b] = proj_psum.tile([P, HEAD_PAIRS, P], F32, name="kv_bank", tag="proj_bank")
+                second_product(b, kv_banks[b], 0)
+                second_product(b, kv_banks[b], 1)
+
+        b = BATCHES - 1
+        kv_bank = proj_psum.tile([P, HEAD_PAIRS, P], F32, name="kv_bank", tag="proj_bank")
+        second_product(b, kv_bank, 0)
+        codes2[GROUPS - 1] = quantise_kv(grouped2[GROUPS - 1], "kv2")
+        second_product(b, kv_bank, 1)
+        kv, squares = end_copy(kv_bank)
+        norm = end_norm(squares)
+        end_store(b, kv, norm)

@@ -57,7 +57,7 @@ def tile_ufoattention_pa_kernel(tc, queries, Wk, bk, Wv, bv, gamma, out):
         nc.vector.memset(ones[:], 1.0)
         ident = consts.tile([P, P], F32, name="ident")
         make_identity(nc, ident[:])
-        nc.scalar.activation(out=warm[:], in_=warm[:], func=ACT.Sqrt)
+        nc.scalar.activation(out=warm[:], in_=warm[:], func=ACT.Abs_reciprocal_sqrt)
         for i, b_vec in enumerate((bk, bv)):
             nc.scalar.dma_start(
                 out=bias_row[0:1, i * FEATURES : (i + 1) * FEATURES],
@@ -69,7 +69,8 @@ def tile_ufoattention_pa_kernel(tc, queries, Wk, bk, Wv, bv, gamma, out):
         w_raw = []
         for g in range(GROUPS):
             x_sb = x_pool.tile([P, PACK * D_MODEL], BF16, name="x_sb")
-            nc.sync.dma_start(out=x_sb[:], in_=x_groups[g])
+            for cols in ((slice(0, 2 * D_MODEL), slice(2 * D_MODEL, 4 * D_MODEL)) if g == 0 else (slice(0, 4 * D_MODEL),)):
+                nc.sync.dma_start(out=x_sb[:, cols], in_=x_groups[g][:, cols])
             x_tiles.append(x_sb)
             if g == 0:
                 for w_name, w in (("wk_raw", Wk), ("wv_raw", Wv)):
@@ -79,57 +80,26 @@ def tile_ufoattention_pa_kernel(tc, queries, Wk, bk, Wv, bv, gamma, out):
         gamma_all = consts.tile([P, HEADS], BF16, name="gamma_all")
         nc.sync.dma_start(out=gamma_all[:], in_=gamma.rearrange("a h b c -> (a h b c)").partition_broadcast(P))
 
-        def transpose_group(g):
+        xt_grouped = {}
+
+        def turn_x(g, u):
             x_words = x_tiles[g][:].bitcast(F32).rearrange("p (j s q) -> p j s q", j=PACK, s=2)
-            banks = []
-            for u in range(2):
-                bank = tr_psum.tile([P, PACK, P], F32, name="xt_bank", tag="tr_bank")
-                for e in range(2):
-                    for s in range(2):
-                        nc.tensor.transpose(bank[:, 2 * e + s, :], x_words[:, 2 * u + e, s, :], ident[:])
-                banks.append(bank)
-            return banks
+            if u == 0:
+                xt_grouped[g] = xt_pool.tile([P, PACK * K_PASS], BF16, name="xt_grouped", align_bytes=64)
+            words = xt_grouped[g][:].bitcast(F32).rearrange("q (u p f) -> q u p f", u=2, f=PACK)
+            bank = tr_psum.tile([P, PACK, P], F32, name="xt_bank", tag="tr_bank")
+            for e in range(2):
+                for s in range(2):
+                    nc.tensor.transpose(bank[:, 2 * e + s, :], x_words[:, 2 * u + e, s, :], ident[:])
+            nc.scalar.copy(out=words[:, u, :, :], in_=bank[:].rearrange("q f p -> q p f"))
 
-        def copy_group(banks):
-            xt_grouped = xt_pool.tile([P, PACK * K_PASS], BF16, name="xt_grouped", align_bytes=64)
-            words = xt_grouped[:].bitcast(F32).rearrange("q (u p f) -> q u p f", u=2, f=PACK)
-            for u in range(2):
-                nc.scalar.copy(out=words[:, u, :, :], in_=banks[u][:].rearrange("q f p -> q p f"))
-            return xt_grouped
-
-        def quantise_x(xt_grouped):
+        def quantise_x(g):
             x_codes = xt_pool.tile([P, K_PASS], U32, name="x_codes", align_bytes=64)
             x_scales = xt_pool.tile([P, K_PASS], U8, name="x_scales", align_bytes=64)
-            nc.vector.quantize_mx(out=x_codes[:].bitcast(FP8X4), scales=x_scales[:], in_=xt_grouped[:])
-            return x_codes, x_scales
+            nc.vector.quantize_mx(out=x_codes[:].bitcast(FP8X4), scales=x_scales[:], in_=xt_grouped[g][:])
+            xq[g] = (x_codes, x_scales)
 
         xq = {}
-        xt0 = copy_group(transpose_group(0))
-
-        w_codes = consts.tile([P, 2, FEATURES], U32, name="w_codes", align_bytes=64)
-        w_scales = consts.tile([P, 2, FEATURES], U8, name="w_scales", align_bytes=64)
-        w_grouped = []
-        for i, w_name in enumerate(("wk_grouped", "wv_grouped")):
-            w_grouped.append(consts.tile([P, FEATURES, PACK], BF16, name=w_name, align_bytes=64))
-
-        def regroup_w(copy, i, lo, hi):
-            copy(
-                out=w_grouped[i][:, lo:hi, :].rearrange("p (c i) t -> p c t i", i=PACK),
-                in_=w_raw[i][:].rearrange("p s e n -> p (s e) n")[:, :, lo:hi].rearrange("p t (c i) -> p c t i", i=PACK),
-            )
-
-        def quantise_w(i):
-            nc.vector.quantize_mx(
-                out=w_codes[:, i, :].bitcast(FP8X4),
-                scales=w_scales[:, i, :],
-                in_=w_grouped[i][:].rearrange("p n t -> p (n t)"),
-            )
-
-        regroup_w(nc.vector.tensor_copy, 0, 0, FEATURES)
-        xq[0] = quantise_x(xt0)
-        quantise_w(0)
-        regroup_w(nc.scalar.copy, 1, HALF, FEATURES)
-        regroup_w(nc.vector.tensor_copy, 1, 0, HALF)
 
         bias_bank = proj_psum.tile([P, 2, HALF], F32, name="bias_bank", tag="proj_bank")
         for i in range(2):
@@ -151,9 +121,35 @@ def tile_ufoattention_pa_kernel(tc, queries, Wk, bk, Wv, bv, gamma, out):
         bias_col = consts.tile([P, PACK], F32, name="bias_col")
         nc.scalar.copy(out=bias_col[:], in_=col_bank[:, :, 0])
 
-        xt1 = copy_group(transpose_group(1))
-        quantise_w(1)
-        xq[1] = quantise_x(xt1)
+        turn_x(0, 0)
+        turn_x(0, 1)
+
+        w_codes = consts.tile([P, 2, FEATURES], U32, name="w_codes", align_bytes=64)
+        w_scales = consts.tile([P, 2, FEATURES], U8, name="w_scales", align_bytes=64)
+        w_grouped = []
+        for i, w_name in enumerate(("wk_grouped", "wv_grouped")):
+            w_grouped.append(consts.tile([P, FEATURES, PACK], BF16, name=w_name, align_bytes=64))
+
+        def regroup_w(copy, i, lo, hi):
+            copy(
+                out=w_grouped[i][:, lo:hi, :].rearrange("p (c i) t -> p c t i", i=PACK),
+                in_=w_raw[i][:].rearrange("p s e n -> p (s e) n")[:, :, lo:hi].rearrange("p t (c i) -> p c t i", i=PACK),
+            )
+
+        def quantise_w(i):
+            nc.vector.quantize_mx(
+                out=w_codes[:, i, :].bitcast(FP8X4),
+                scales=w_scales[:, i, :],
+                in_=w_grouped[i][:].rearrange("p n t -> p (n t)"),
+            )
+
+        for i in range(2):
+            regroup_w(nc.vector.tensor_copy, i, HALF, FEATURES)
+            regroup_w(nc.scalar.copy, i, 0, HALF)
+            if i == 0:
+                quantise_x(0)
+            quantise_w(i)
+        turn_x(1, 0)
 
         grouped1 = {}
         grouped2 = {}
@@ -202,22 +198,15 @@ def tile_ufoattention_pa_kernel(tc, queries, Wk, bk, Wv, bv, gamma, out):
                 op=ALU.add,
             )
 
-        def transpose_back(g):
-            banks = []
-            for pair in range(WAY_PAIRS):
-                bank = tr_psum.tile([P, 2, 2, P], F32, name="tok_bank", tag="tr_bank")
-                for i in range(2):
-                    words = feats[g, pair, i][:].bitcast(F32)
-                    for u in range(2):
-                        nc.tensor.transpose(bank[:, i, u, :], words[:, u * P : (u + 1) * P], ident[:])
-                banks.append(bank)
-            return banks
-
-        def copy_back(g, banks):
-            for pair in range(WAY_PAIRS):
-                words = grouped2[g][:].rearrange("p a i f t -> p (a i f t)").bitcast(F32)
-                words = words.rearrange("p (a i f u) -> p a i f u", a=WAY_PAIRS, i=2, u=2)
-                nc.scalar.copy(out=words[:, pair, :, :, :], in_=banks[pair][:].rearrange("p i u f -> p i f u"))
+        def turn_back(g, pair, copy):
+            bank = tr_psum.tile([P, 2, 2, P], F32, name="tok_bank", tag="tr_bank")
+            for i in range(2):
+                words = feats[g, pair, i][:].bitcast(F32)
+                for u in range(2):
+                    nc.tensor.transpose(bank[:, i, u, :], words[:, u * P : (u + 1) * P], ident[:])
+            words = grouped2[g][:].rearrange("p a i f t -> p (a i f t)").bitcast(F32)
+            words = words.rearrange("p (a i f u) -> p a i f u", a=WAY_PAIRS, i=2, u=2)
+            copy(out=words[:, pair, :, :, :], in_=bank[:].rearrange("p i u f -> p i f u"))
 
         def quantise_kv(grouped, name):
             codes = kvq_pool.tile([P, WAY_PAIRS, 2, P], U32, name=name + "_codes", align_bytes=64)
@@ -251,72 +240,92 @@ def tile_ufoattention_pa_kernel(tc, queries, Wk, bk, Wv, bv, gamma, out):
             nc.gpsimd.tensor_copy(out=gain[0:D_HEAD, :], in_=gamma_by_half[0:D_HEAD, 0, :])
             nc.gpsimd.tensor_copy(out=gain[D_HEAD:P, :], in_=gamma_by_half[D_HEAD:P, 1, :])
 
-        ends = {}
+        def end_copy(kv_bank, lo, hi):
+            kv = end_pool.tile([P, hi - lo, D_HEAD], F32, name="kv")
+            nc.scalar.copy(out=kv[0:D_HEAD, :, :], in_=kv_bank[0:D_HEAD, lo:hi, 0:D_HEAD])
+            nc.vector.tensor_copy(out=kv[D_HEAD:P, :, :], in_=kv_bank[D_HEAD:P, lo:hi, D_HEAD:P])
+            return kv
 
-        def end_copy(kv_bank):
-            kv = end_pool.tile([P, HEAD_PAIRS, D_HEAD], F32, name="kv")
-            nc.scalar.copy(out=kv[0:D_HEAD, :, :], in_=kv_bank[0:D_HEAD, :, 0:D_HEAD])
-            nc.vector.tensor_copy(out=kv[D_HEAD:P, :, :], in_=kv_bank[D_HEAD:P, :, D_HEAD:P])
-            squares = end_pool.tile([P, HEAD_PAIRS, D_HEAD], F32, name="squares")
-            nc.gpsimd.tensor_tensor(out=squares[:], in0=kv[:], in1=kv[:], op=ALU.mult)
-            return kv, squares
-
-        def end_norm(squares):
-            total = end_pool.tile([P, HEAD_PAIRS], F32, name="total")
+        def end_norm(kv, squares_engine):
+            pairs = kv.shape[1]
+            squares = end_pool.tile([P, pairs, D_HEAD], F32, name="squares")
+            squares_engine.tensor_tensor(out=squares[:], in0=kv[:], in1=kv[:], op=ALU.mult)
+            total = end_pool.tile([P, pairs], F32, name="total")
             nc.vector.tensor_reduce(out=total[:], in_=squares[:], axis=AX.X, op=ALU.add)
-            norm = end_pool.tile([P, HEAD_PAIRS], F32, name="norm")
-            nc.scalar.activation(out=norm[:], in_=total[:], func=ACT.Sqrt)
-            return norm
+            inverse = end_pool.tile([P, pairs], F32, name="inverse")
+            nc.scalar.activation(out=inverse[:], in_=total[:], func=ACT.Abs_reciprocal_sqrt)
+            return inverse
 
-        def end_store(b, kv, norm):
-            factor = end_pool.tile([P, HEAD_PAIRS], F32, name="factor")
-            nc.vector.reciprocal(out=factor[:], in_=norm[:])
-            nc.gpsimd.tensor_tensor(out=factor[:], in0=factor[:], in1=gain[:], op=ALU.mult)
-            result = end_pool.tile([P, HEAD_PAIRS, D_HEAD], F32, name="result")
-            nc.gpsimd.tensor_tensor(
+        def end_store(b, lo, kv, inverse, engine):
+            pairs = kv.shape[1]
+            factor = end_pool.tile([P, pairs], F32, name="factor")
+            engine.tensor_tensor(out=factor[:], in0=inverse[:], in1=gain[:, lo : lo + pairs], op=ALU.mult)
+            result = end_pool.tile([P, pairs, D_HEAD], F32, name="result")
+            engine.tensor_tensor(
                 out=result[:],
                 in0=kv[:],
-                in1=factor[:].unsqueeze(2).to_broadcast([P, HEAD_PAIRS, D_HEAD]),
+                in1=factor[:].unsqueeze(2).to_broadcast([P, pairs, D_HEAD]),
                 op=ALU.mult,
             )
-            nc.sync.dma_start(out=out[b].rearrange("(pair half) i j -> (half i) pair j", half=2), in_=result[:])
+            nc.sync.dma_start(
+                out=out[b].rearrange("(pair half) i j -> (half i) pair j", half=2)[:, lo : lo + pairs, :], in_=result[:]
+            )
 
-        kv_banks = {}
+        def second_products(b):
+            bank = proj_psum.tile([P, HEAD_PAIRS, P], F32, name="kv_bank", tag="proj_bank")
+            second_product(b, bank, 0)
+            second_product(b, bank, 1)
+            return bank
+
         for g in range(GROUPS):
-            ending = g // 2 - 1 if g % 2 == 1 and g > 1 else None
+            ending = (g - 3) // 2 if g % 2 == 1 and g > 1 else None
             grouped1[g] = kv_pool.tile([P, WAY_PAIRS, 2, P, PACK], BF16, name="kv_grouped1", align_bytes=64)
             grouped2[g] = kv_pool.tile([P, WAY_PAIRS, 2, P, PACK], BF16, name="kv_grouped2", align_bytes=64)
-            for n in range(4):
+
+            for n in (0, 1):
                 way2_tile(g, n)
                 way1_tile(g, n)
-                if ending is not None:
-                    if n == 0:
-                        if ending == 0:
-                            load_gain()
-                        kv, squares = end_copy(kv_banks[ending])
-                    elif n == 2:
-                        norm = end_norm(squares)
-                    elif n == 3:
-                        end_store(ending, kv, norm)
-            if g + 2 < GROUPS:
-                xt = copy_group(transpose_group(g + 2))
+            if ending is not None:
+                kv_bank = second_products(ending)
+            unit = 2 * g + 3
+            if unit < 2 * GROUPS:
+                turn_x(unit // 2, unit % 2)
+            if g > 0:
+                turn_back(g - 1, 1, nc.scalar.copy)
+                codes1[g - 1] = quantise_kv(grouped1[g - 1], "kv1")
+
+            way2_tile(g, 2)
+            way1_tile(g, 2)
+            if g + 1 < GROUPS:
+                quantise_x(g + 1)
+            if ending is not None:
+                kv = end_copy(kv_bank, 0, HEAD_PAIRS)
+            way2_tile(g, 3)
+            way1_tile(g, 3)
+            unit = 2 * g + 4
+            if unit < 2 * GROUPS:
+                turn_x(unit // 2, unit % 2)
+            turn_back(g, 0, nc.scalar.copy)
             if g > 0:
                 codes2[g - 1] = quantise_kv(grouped2[g - 1], "kv2")
-            codes1[g] = quantise_kv(grouped1[g], "kv1")
-            copy_back(g, transpose_back(g))
-            if g + 2 < GROUPS:
-                xq[g + 2] = quantise_x(xt)
-            if g % 2 == 0 and g > 0:
-                b = g // 2 - 1
-                kv_banks[b] = proj_psum.tile([P, HEAD_PAIRS, P], F32, name="kv_bank", tag="proj_bank")
-                second_product(b, kv_banks[b], 0)
-                second_product(b, kv_banks[b], 1)
+            if ending is not None:
+                if ending == 0:
+                    load_gain()
+                inverse = end_norm(kv, nc.gpsimd)
+                end_store(ending, 0, kv, inverse, nc.gpsimd)
 
+        g = GROUPS - 1
+        turn_back(g, 1, nc.scalar.copy)
+        codes1[g] = quantise_kv(grouped1[g], "kv1")
         b = BATCHES - 1
         kv_bank = proj_psum.tile([P, HEAD_PAIRS, P], F32, name="kv_bank", tag="proj_bank")
         second_product(b, kv_bank, 0)
-        codes2[GROUPS - 1] = quantise_kv(grouped2[GROUPS - 1], "kv2")
-        second_product(b, kv_bank, 1)
-        kv, squares = end_copy(kv_bank)
-        norm = end_norm(squares)
-        end_store(b, kv, norm)
+        codes2[g] = quantise_kv(grouped2[g], "kv2")
+        kv_low = end_copy(kv_bank, 0, WAY_PAIRS)
+        inverse = end_norm(kv_low, nc.vector)
+        end_store(b, 0, kv_low, inverse, nc.gpsimd)
+        kv_bank2 = proj_psum.tile([P, HEAD_PAIRS, P], F32, name="kv_bank", tag="proj_bank")
+        second_product(b, kv_bank2, 1)
+        kv_high = end_copy(kv_bank2, WAY_PAIRS, HEAD_PAIRS)
+        inverse = end_norm(kv_high, nc.vector)
+        end_store(b, WAY_PAIRS, kv_high, inverse, nc.vector)

@@ -58,20 +58,24 @@ def tile_ufoattention_pa_kernel(tc, queries, Wk, bk, Wv, bv, gamma, out):
         ident = consts.tile([P, P], F32, name="ident")
         make_identity(nc, ident[:])
         nc.scalar.activation(out=warm[:], in_=warm[:], func=ACT.Abs_reciprocal_sqrt)
-        for i, b_vec in enumerate((bk, bv)):
-            nc.scalar.dma_start(
-                out=bias_row[0:1, i * FEATURES : (i + 1) * FEATURES],
-                in_=b_vec.rearrange("(o n) -> o n", o=1),
-            )
-
         x_groups = queries.flatten_outer_dims().rearrange("(g p j) d -> g p (j d)", p=P, j=PACK)
         x_tiles = []
         w_raw = []
         for g in range(GROUPS):
             x_sb = x_pool.tile([P, PACK * D_MODEL], BF16, name="x_sb")
-            for cols in ((slice(0, 2 * D_MODEL), slice(2 * D_MODEL, 4 * D_MODEL)) if g == 0 else (slice(0, 4 * D_MODEL),)):
-                nc.sync.dma_start(out=x_sb[:, cols], in_=x_groups[g][:, cols])
             x_tiles.append(x_sb)
+            if g > 0:
+                nc.sync.dma_start(out=x_sb[:], in_=x_groups[g])
+            else:
+                half = slice(0, 2 * D_MODEL)
+                nc.sync.dma_start(out=x_sb[:, half], in_=x_groups[g][:, half])
+                for i, b_vec in enumerate((bk, bv)):
+                    nc.sync.dma_start(
+                        out=bias_row[0:1, i * FEATURES : (i + 1) * FEATURES],
+                        in_=b_vec.rearrange("(o n) -> o n", o=1),
+                    )
+                half = slice(2 * D_MODEL, 4 * D_MODEL)
+                nc.sync.dma_start(out=x_sb[:, half], in_=x_groups[g][:, half])
             if g == 0:
                 for w_name, w in (("wk_raw", Wk), ("wv_raw", Wv)):
                     raw = consts.tile([P, 2, 2, FEATURES], BF16, name=w_name)
@@ -144,8 +148,11 @@ def tile_ufoattention_pa_kernel(tc, queries, Wk, bk, Wv, bv, gamma, out):
             )
 
         for i in range(2):
-            regroup_w(nc.vector.tensor_copy, i, HALF, FEATURES)
-            regroup_w(nc.scalar.copy, i, 0, HALF)
+            if i == 0:
+                regroup_w(nc.vector.tensor_copy, i, HALF, FEATURES)
+                regroup_w(nc.scalar.copy, i, 0, HALF)
+            else:
+                regroup_w(nc.vector.tensor_copy, i, 0, FEATURES)
             if i == 0:
                 quantise_x(0)
             quantise_w(i)
@@ -246,10 +253,13 @@ def tile_ufoattention_pa_kernel(tc, queries, Wk, bk, Wv, bv, gamma, out):
             nc.vector.tensor_copy(out=kv[D_HEAD:P, :, :], in_=kv_bank[D_HEAD:P, lo:hi, D_HEAD:P])
             return kv
 
-        def end_norm(kv, squares_engine):
-            pairs = kv.shape[1]
-            squares = end_pool.tile([P, pairs, D_HEAD], F32, name="squares")
-            squares_engine.tensor_tensor(out=squares[:], in0=kv[:], in1=kv[:], op=ALU.mult)
+        def end_square(kv, engine):
+            squares = end_pool.tile([P, kv.shape[1], D_HEAD], F32, name="squares")
+            engine.tensor_tensor(out=squares[:], in0=kv[:], in1=kv[:], op=ALU.mult)
+            return squares
+
+        def end_norm(squares):
+            pairs = squares.shape[1]
             total = end_pool.tile([P, pairs], F32, name="total")
             nc.vector.tensor_reduce(out=total[:], in_=squares[:], axis=AX.X, op=ALU.add)
             inverse = end_pool.tile([P, pairs], F32, name="inverse")
@@ -282,11 +292,15 @@ def tile_ufoattention_pa_kernel(tc, queries, Wk, bk, Wv, bv, gamma, out):
             grouped1[g] = kv_pool.tile([P, WAY_PAIRS, 2, P, PACK], BF16, name="kv_grouped1", align_bytes=64)
             grouped2[g] = kv_pool.tile([P, WAY_PAIRS, 2, P, PACK], BF16, name="kv_grouped2", align_bytes=64)
 
-            for n in (0, 1):
-                way2_tile(g, n)
-                way1_tile(g, n)
+            way2_tile(g, 0)
+            way1_tile(g, 0)
             if ending is not None:
                 kv_bank = second_products(ending)
+            way2_tile(g, 1)
+            way1_tile(g, 1)
+            if ending is not None:
+                kv = end_copy(kv_bank, 0, HEAD_PAIRS)
+                squares = end_square(kv, nc.gpsimd)
             unit = 2 * g + 3
             if unit < 2 * GROUPS:
                 turn_x(unit // 2, unit % 2)
@@ -298,8 +312,6 @@ def tile_ufoattention_pa_kernel(tc, queries, Wk, bk, Wv, bv, gamma, out):
             way1_tile(g, 2)
             if g + 1 < GROUPS:
                 quantise_x(g + 1)
-            if ending is not None:
-                kv = end_copy(kv_bank, 0, HEAD_PAIRS)
             way2_tile(g, 3)
             way1_tile(g, 3)
             unit = 2 * g + 4
@@ -311,7 +323,7 @@ def tile_ufoattention_pa_kernel(tc, queries, Wk, bk, Wv, bv, gamma, out):
             if ending is not None:
                 if ending == 0:
                     load_gain()
-                inverse = end_norm(kv, nc.gpsimd)
+                inverse = end_norm(squares)
                 end_store(ending, 0, kv, inverse, nc.gpsimd)
 
         g = GROUPS - 1
@@ -322,10 +334,10 @@ def tile_ufoattention_pa_kernel(tc, queries, Wk, bk, Wv, bv, gamma, out):
         second_product(b, kv_bank, 0)
         codes2[g] = quantise_kv(grouped2[g], "kv2")
         kv_low = end_copy(kv_bank, 0, WAY_PAIRS)
-        inverse = end_norm(kv_low, nc.vector)
+        inverse = end_norm(end_square(kv_low, nc.vector))
         end_store(b, 0, kv_low, inverse, nc.gpsimd)
         kv_bank2 = proj_psum.tile([P, HEAD_PAIRS, P], F32, name="kv_bank", tag="proj_bank")
         second_product(b, kv_bank2, 1)
         kv_high = end_copy(kv_bank2, WAY_PAIRS, HEAD_PAIRS)
-        inverse = end_norm(kv_high, nc.vector)
+        inverse = end_norm(end_square(kv_high, nc.vector))
         end_store(b, WAY_PAIRS, kv_high, inverse, nc.vector)

@@ -60,27 +60,27 @@ def tile_ufoattention_pa_kernel(tc, queries, Wk, bk, Wv, bv, gamma, out):
         nc.scalar.activation(out=warm[:], in_=warm[:], func=ACT.Abs_reciprocal_sqrt)
         x_groups = queries.flatten_outer_dims().rearrange("(g p j) d -> g p (j d)", p=P, j=PACK)
         x_tiles = []
-        w_raw = []
         for g in range(GROUPS):
-            x_sb = x_pool.tile([P, PACK * D_MODEL], BF16, name="x_sb")
-            x_tiles.append(x_sb)
-            if g > 0:
-                nc.sync.dma_start(out=x_sb[:], in_=x_groups[g])
-            else:
-                half = slice(0, 2 * D_MODEL)
-                nc.sync.dma_start(out=x_sb[:, half], in_=x_groups[g][:, half])
-                for i, b_vec in enumerate((bk, bv)):
-                    nc.sync.dma_start(
-                        out=bias_row[0:1, i * FEATURES : (i + 1) * FEATURES],
-                        in_=b_vec.rearrange("(o n) -> o n", o=1),
-                    )
-                half = slice(2 * D_MODEL, 4 * D_MODEL)
-                nc.sync.dma_start(out=x_sb[:, half], in_=x_groups[g][:, half])
-            if g == 0:
-                for w_name, w in (("wk_raw", Wk), ("wv_raw", Wv)):
-                    raw = consts.tile([P, 2, 2, FEATURES], BF16, name=w_name)
-                    nc.sync.dma_start(out=raw[:], in_=w.rearrange("(s q e) n -> q s e n", s=2, e=2))
-                    w_raw.append(raw)
+            x_tiles.append(x_pool.tile([P, PACK * D_MODEL], BF16, name="x_sb"))
+        w_raw = []
+        for w_name in ("wk_raw", "wv_raw"):
+            w_raw.append(consts.tile([P, 2, 2, FEATURES], BF16, name=w_name))
+
+        def load_x(g, lo, hi):
+            nc.sync.dma_start(
+                out=x_tiles[g][:, lo * D_MODEL : hi * D_MODEL], in_=x_groups[g][:, lo * D_MODEL : hi * D_MODEL]
+            )
+
+        load_x(0, 0, 2)
+        for i, b_vec in enumerate((bk, bv)):
+            nc.sync.dma_start(
+                out=bias_row[0:1, i * FEATURES : (i + 1) * FEATURES], in_=b_vec.rearrange("(o n) -> o n", o=1)
+            )
+        nc.sync.dma_start(out=w_raw[0][:], in_=Wk.rearrange("(s q e) n -> q s e n", s=2, e=2))
+        load_x(0, 2, 4)
+        nc.sync.dma_start(out=w_raw[1][:], in_=Wv.rearrange("(s q e) n -> q s e n", s=2, e=2))
+        for g in range(1, GROUPS):
+            load_x(g, 0, 4)
         gamma_all = consts.tile([P, HEADS], BF16, name="gamma_all")
         nc.sync.dma_start(out=gamma_all[:], in_=gamma.rearrange("a h b c -> (a h b c)").partition_broadcast(P))
 
@@ -105,6 +105,8 @@ def tile_ufoattention_pa_kernel(tc, queries, Wk, bk, Wv, bv, gamma, out):
 
         xq = {}
 
+        turn_x(0, 0)
+
         bias_bank = proj_psum.tile([P, 2, HALF], F32, name="bias_bank", tag="proj_bank")
         for i in range(2):
             nc.tensor.matmul(
@@ -125,7 +127,6 @@ def tile_ufoattention_pa_kernel(tc, queries, Wk, bk, Wv, bv, gamma, out):
         bias_col = consts.tile([P, PACK], F32, name="bias_col")
         nc.scalar.copy(out=bias_col[:], in_=col_bank[:, :, 0])
 
-        turn_x(0, 0)
         turn_x(0, 1)
 
         w_codes = consts.tile([P, 2, FEATURES], U32, name="w_codes", align_bytes=64)
@@ -147,16 +148,12 @@ def tile_ufoattention_pa_kernel(tc, queries, Wk, bk, Wv, bv, gamma, out):
                 in_=w_grouped[i][:].rearrange("p n t -> p (n t)"),
             )
 
-        for i in range(2):
-            if i == 0:
-                regroup_w(nc.vector.tensor_copy, i, HALF, FEATURES)
-                regroup_w(nc.scalar.copy, i, 0, HALF)
-            else:
-                regroup_w(nc.vector.tensor_copy, i, 0, FEATURES)
-            if i == 0:
-                quantise_x(0)
-            quantise_w(i)
-        turn_x(1, 0)
+        regroup_w(nc.vector.tensor_copy, 0, 0, FEATURES)
+        quantise_w(0)
+        quantise_x(0)
+        regroup_w(nc.scalar.copy, 1, HALF, FEATURES)
+        regroup_w(nc.vector.tensor_copy, 1, 0, HALF)
+        quantise_w(1)
 
         grouped1 = {}
         grouped2 = {}
@@ -247,36 +244,39 @@ def tile_ufoattention_pa_kernel(tc, queries, Wk, bk, Wv, bv, gamma, out):
             nc.gpsimd.tensor_copy(out=gain[0:D_HEAD, :], in_=gamma_by_half[0:D_HEAD, 0, :])
             nc.gpsimd.tensor_copy(out=gain[D_HEAD:P, :], in_=gamma_by_half[D_HEAD:P, 1, :])
 
-        def end_copy(kv_bank, lo, hi):
+        def end_copy(kv_bank, lo, hi, copy_low, copy_high):
             kv = end_pool.tile([P, hi - lo, D_HEAD], F32, name="kv")
-            nc.scalar.copy(out=kv[0:D_HEAD, :, :], in_=kv_bank[0:D_HEAD, lo:hi, 0:D_HEAD])
-            nc.vector.tensor_copy(out=kv[D_HEAD:P, :, :], in_=kv_bank[D_HEAD:P, lo:hi, D_HEAD:P])
+            copy_low(out=kv[0:D_HEAD, :, :], in_=kv_bank[0:D_HEAD, lo:hi, 0:D_HEAD])
+            copy_high(out=kv[D_HEAD:P, :, :], in_=kv_bank[D_HEAD:P, lo:hi, D_HEAD:P])
             return kv
 
-        def end_square(kv, engine):
-            squares = end_pool.tile([P, kv.shape[1], D_HEAD], F32, name="squares")
-            engine.tensor_tensor(out=squares[:], in0=kv[:], in1=kv[:], op=ALU.mult)
-            return squares
-
-        def end_norm(squares):
-            pairs = squares.shape[1]
-            total = end_pool.tile([P, pairs], F32, name="total")
-            nc.vector.tensor_reduce(out=total[:], in_=squares[:], axis=AX.X, op=ALU.add)
-            inverse = end_pool.tile([P, pairs], F32, name="inverse")
+        def end_inverse(total):
+            inverse = end_pool.tile([P, total.shape[1]], F32, name="inverse")
             nc.scalar.activation(out=inverse[:], in_=total[:], func=ACT.Abs_reciprocal_sqrt)
             return inverse
 
-        def end_store(b, lo, kv, inverse, engine):
+        def end_square(kv):
             pairs = kv.shape[1]
-            factor = end_pool.tile([P, pairs], F32, name="factor")
-            engine.tensor_tensor(out=factor[:], in0=inverse[:], in1=gain[:, lo : lo + pairs], op=ALU.mult)
+            squares = end_pool.tile([P, pairs, D_HEAD], F32, name="squares")
+            total = end_pool.tile([P, pairs], F32, name="total")
+            for i in range(pairs):
+                nc.scalar.activation(
+                    out=squares[:, i, :], in_=kv[:, i, :], func=ACT.Square, accum_out=total[:, i : i + 1]
+                )
+            return total
+
+        def end_store(b, lo, kv, inverse):
+            pairs = kv.shape[1]
             result = end_pool.tile([P, pairs, D_HEAD], F32, name="result")
-            engine.tensor_tensor(
-                out=result[:],
-                in0=kv[:],
-                in1=factor[:].unsqueeze(2).to_broadcast([P, pairs, D_HEAD]),
-                op=ALU.mult,
-            )
+            for i in range(pairs):
+                nc.vector.tensor_scalar(
+                    out=result[:, i, :],
+                    in0=kv[:, i, :],
+                    scalar1=inverse[:, i : i + 1],
+                    scalar2=gain[:, lo + i : lo + i + 1],
+                    op0=ALU.mult,
+                    op1=ALU.mult,
+                )
             nc.sync.dma_start(
                 out=out[b].rearrange("(pair half) i j -> (half i) pair j", half=2)[:, lo : lo + pairs, :], in_=result[:]
             )
@@ -289,29 +289,46 @@ def tile_ufoattention_pa_kernel(tc, queries, Wk, bk, Wv, bv, gamma, out):
 
         for g in range(GROUPS):
             ending = (g - 3) // 2 if g % 2 == 1 and g > 1 else None
+            storing = (g - 4) // 2 if g % 2 == 0 and g > 2 else None
+            last_end = ending == BATCHES - 2
             grouped1[g] = kv_pool.tile([P, WAY_PAIRS, 2, P, PACK], BF16, name="kv_grouped1", align_bytes=64)
             grouped2[g] = kv_pool.tile([P, WAY_PAIRS, 2, P, PACK], BF16, name="kv_grouped2", align_bytes=64)
 
             way2_tile(g, 0)
             way1_tile(g, 0)
+            if g == 0:
+                turn_x(1, 0)
             if ending is not None:
                 kv_bank = second_products(ending)
+            if storing is not None:
+                total = end_pool.tile([P, HEAD_PAIRS], F32, name="total")
+                nc.vector.tensor_reduce(out=total[:], in_=squares[:], axis=AX.X, op=ALU.add)
             way2_tile(g, 1)
             way1_tile(g, 1)
             if ending is not None:
-                kv = end_copy(kv_bank, 0, HEAD_PAIRS)
-                squares = end_square(kv, nc.gpsimd)
+                kv = end_copy(
+                    kv_bank, 0, HEAD_PAIRS, nc.scalar.copy, nc.scalar.copy if last_end else nc.vector.tensor_copy
+                )
+            if storing is not None:
+                inverse = end_inverse(total)
             unit = 2 * g + 3
             if unit < 2 * GROUPS:
                 turn_x(unit // 2, unit % 2)
             if g > 0:
                 turn_back(g - 1, 1, nc.scalar.copy)
                 codes1[g - 1] = quantise_kv(grouped1[g - 1], "kv1")
+            if ending is not None and not last_end:
+                squares = end_pool.tile([P, HEAD_PAIRS, D_HEAD], F32, name="squares")
+                nc.vector.tensor_tensor(out=squares[:], in0=kv[:], in1=kv[:], op=ALU.mult)
+            if storing is not None:
+                end_store(storing, 0, kv, inverse)
 
             way2_tile(g, 2)
             way1_tile(g, 2)
             if g + 1 < GROUPS:
                 quantise_x(g + 1)
+            if g == 3:
+                load_gain()
             way2_tile(g, 3)
             way1_tile(g, 3)
             unit = 2 * g + 4
@@ -320,24 +337,38 @@ def tile_ufoattention_pa_kernel(tc, queries, Wk, bk, Wv, bv, gamma, out):
             turn_back(g, 0, nc.scalar.copy)
             if g > 0:
                 codes2[g - 1] = quantise_kv(grouped2[g - 1], "kv2")
-            if ending is not None:
-                if ending == 0:
-                    load_gain()
-                inverse = end_norm(squares)
-                end_store(ending, 0, kv, inverse, nc.gpsimd)
 
         g = GROUPS - 1
-        turn_back(g, 1, nc.scalar.copy)
-        codes1[g] = quantise_kv(grouped1[g], "kv1")
         b = BATCHES - 1
+        words = grouped2[g][:].rearrange("p a i f t -> p (a i f t)").bitcast(F32)
+        words = words.rearrange("p (a i f u) -> p a i f u", a=WAY_PAIRS, i=2, u=2)
+        codes1[g] = quantise_kv(grouped1[g], "kv1")
+        for i in range(2):
+            bank = tr_psum.tile([P, 2, P], F32, name="last_bank", tag="tr_bank")
+            feat_words = feats[g, 1, i][:].bitcast(F32)
+            for u in range(2):
+                nc.tensor.transpose(bank[:, u, :], feat_words[:, u * P : (u + 1) * P], ident[:])
+            nc.scalar.copy(out=words[:, 1, i, :, :], in_=bank[:].rearrange("p u f -> p f u"))
+        inverse = end_inverse(end_square(kv))
         kv_bank = proj_psum.tile([P, HEAD_PAIRS, P], F32, name="kv_bank", tag="proj_bank")
         second_product(b, kv_bank, 0)
-        codes2[g] = quantise_kv(grouped2[g], "kv2")
-        kv_low = end_copy(kv_bank, 0, WAY_PAIRS)
-        inverse = end_norm(end_square(kv_low, nc.vector))
-        end_store(b, 0, kv_low, inverse, nc.gpsimd)
+        codes = kvq_pool.tile([P, WAY_PAIRS, 2, P], U32, name="kv2_codes", align_bytes=64)
+        scales = kvq_pool.tile([P, WAY_PAIRS, 2, P], U8, name="kv2_scales", align_bytes=64)
+        for pair in range(WAY_PAIRS):
+            nc.vector.quantize_mx(
+                out=codes[:, pair, :, :].rearrange("p i f -> p (i f)").bitcast(FP8X4),
+                scales=scales[:, pair, :, :].rearrange("p i f -> p (i f)"),
+                in_=grouped2[g][:, pair, :, :, :].rearrange("p i f t -> p (i f t)"),
+            )
+        codes2[g] = (codes, scales)
+        end_store(b - 1, 0, kv, inverse)
+        kv_low = end_copy(kv_bank, 0, WAY_PAIRS, nc.scalar.copy, nc.scalar.copy)
+        total_low = end_square(kv_low)
+        inverse_low = end_inverse(total_low)
         kv_bank2 = proj_psum.tile([P, HEAD_PAIRS, P], F32, name="kv_bank", tag="proj_bank")
         second_product(b, kv_bank2, 1)
-        kv_high = end_copy(kv_bank2, WAY_PAIRS, HEAD_PAIRS)
-        inverse = end_norm(end_square(kv_high, nc.vector))
-        end_store(b, WAY_PAIRS, kv_high, inverse, nc.vector)
+        kv_high = end_copy(kv_bank2, WAY_PAIRS, HEAD_PAIRS, nc.vector.tensor_copy, nc.vector.tensor_copy)
+        total_high = end_square(kv_high)
+        inverse_high = end_inverse(total_high)
+        end_store(b, 0, kv_low, inverse_low)
+        end_store(b, WAY_PAIRS, kv_high, inverse_high)

@@ -55,6 +55,8 @@ def tile_ufoattention_pa_kernel(tc, queries, Wk, bk, Wv, bv, gamma, out):
         nc.vector.memset(bias_row[:], 0.0)
         ones = consts.tile([P, P], BF16, name="ones")
         nc.vector.memset(ones[:], 1.0)
+        idle_rhs = consts.tile([P, FEATURES], BF16, name="idle_rhs")
+        nc.vector.memset(idle_rhs[:], 0.0)
         ident = consts.tile([P, P], F32, name="ident")
         make_identity(nc, ident[:])
         nc.scalar.activation(out=warm[:], in_=warm[:], func=ACT.Abs_reciprocal_sqrt)
@@ -76,8 +78,8 @@ def tile_ufoattention_pa_kernel(tc, queries, Wk, bk, Wv, bv, gamma, out):
             nc.sync.dma_start(
                 out=bias_row[0:1, i * FEATURES : (i + 1) * FEATURES], in_=b_vec.rearrange("(o n) -> o n", o=1)
             )
-        nc.sync.dma_start(out=w_raw[0][:], in_=Wk.rearrange("(s q e) n -> q s e n", s=2, e=2))
         load_x(0, 2, 4)
+        nc.sync.dma_start(out=w_raw[0][:], in_=Wk.rearrange("(s q e) n -> q s e n", s=2, e=2))
         nc.sync.dma_start(out=w_raw[1][:], in_=Wv.rearrange("(s q e) n -> q s e n", s=2, e=2))
         for g in range(1, GROUPS):
             load_x(g, 0, 4)
@@ -105,7 +107,15 @@ def tile_ufoattention_pa_kernel(tc, queries, Wk, bk, Wv, bv, gamma, out):
 
         xq = {}
 
+        def keep_busy(count):
+            idle_bank = proj_psum.tile([P, FEATURES], F32, name="idle_bank", tag="proj_bank")
+            for i in range(count):
+                nc.tensor.matmul(out=idle_bank[:], lhsT=ones[:], rhs=idle_rhs[:], start=True, stop=True)
+
+        keep_busy(4)
         turn_x(0, 0)
+        turn_x(0, 1)
+        keep_busy(5)
 
         bias_bank = proj_psum.tile([P, 2, HALF], F32, name="bias_bank", tag="proj_bank")
         for i in range(2):
@@ -122,13 +132,6 @@ def tile_ufoattention_pa_kernel(tc, queries, Wk, bk, Wv, bv, gamma, out):
             nc.tensor.matmul(
                 out=col_bank[:, n, :], lhsT=bias_row[:, lo : lo + P], rhs=ones[:, 0:ONES_COLS], start=True, stop=True
             )
-        bias = consts.tile([P, 2, HALF], F32, name="bias")
-        nc.scalar.copy(out=bias[:], in_=bias_bank[:])
-        bias_col = consts.tile([P, PACK], F32, name="bias_col")
-        nc.scalar.copy(out=bias_col[:], in_=col_bank[:, :, 0])
-
-        turn_x(0, 1)
-
         w_codes = consts.tile([P, 2, FEATURES], U32, name="w_codes", align_bytes=64)
         w_scales = consts.tile([P, 2, FEATURES], U8, name="w_scales", align_bytes=64)
         w_grouped = []
@@ -141,19 +144,24 @@ def tile_ufoattention_pa_kernel(tc, queries, Wk, bk, Wv, bv, gamma, out):
                 in_=w_raw[i][:].rearrange("p s e n -> p (s e) n")[:, :, lo:hi].rearrange("p t (c i) -> p c t i", i=PACK),
             )
 
-        def quantise_w(i):
+        def quantise_w(i, lo, hi):
             nc.vector.quantize_mx(
-                out=w_codes[:, i, :].bitcast(FP8X4),
-                scales=w_scales[:, i, :],
-                in_=w_grouped[i][:].rearrange("p n t -> p (n t)"),
+                out=w_codes[:, i, lo:hi].bitcast(FP8X4),
+                scales=w_scales[:, i, lo:hi],
+                in_=w_grouped[i][:, lo:hi, :].rearrange("p n t -> p (n t)"),
             )
 
-        regroup_w(nc.vector.tensor_copy, 0, 0, FEATURES)
-        quantise_w(0)
+        regroup_w(nc.vector.tensor_copy, 0, HALF, FEATURES)
+        regroup_w(nc.scalar.copy, 0, 0, HALF)
         quantise_x(0)
-        regroup_w(nc.scalar.copy, 1, HALF, FEATURES)
-        regroup_w(nc.vector.tensor_copy, 1, 0, HALF)
-        quantise_w(1)
+        bias = consts.tile([P, 2, HALF], F32, name="bias")
+        nc.scalar.copy(out=bias[:], in_=bias_bank[:])
+        bias_col = consts.tile([P, PACK], F32, name="bias_col")
+        nc.scalar.copy(out=bias_col[:], in_=col_bank[:, :, 0])
+        quantise_w(0, HALF, FEATURES)
+        quantise_w(0, 0, HALF)
+        regroup_w(nc.vector.tensor_copy, 1, 0, FEATURES)
+        quantise_w(1, 0, FEATURES)
 
         grouped1 = {}
         grouped2 = {}

@@ -32,6 +32,7 @@ ONES_COLS = 32
 FLOPS = 2 * BATCHES * TOKENS * D_MODEL * 2 * FEATURES + 2 * BATCHES * HEADS * TOKENS * D_HEAD * D_HEAD
 
 TILES = [(0, 0), (1, 0), (0, 1), (1, 1)]
+PAIRWISE = [(0, 0), (0, 1), (1, 0), (1, 1)]
 
 
 def tile_ufoattention_pa_kernel(tc, queries, Wk, bk, Wv, bv, gamma, out):
@@ -43,7 +44,7 @@ def tile_ufoattention_pa_kernel(tc, queries, Wk, bk, Wv, bv, gamma, out):
         kv_pool = ctx.enter_context(tc.tile_pool(name="kv", bufs=2))
         feat_pool = ctx.enter_context(tc.tile_pool(name="feat", bufs=8))
         kvq_pool = ctx.enter_context(tc.tile_pool(name="kvq", bufs=4))
-        end_pool = ctx.enter_context(tc.tile_pool(name="end", bufs=2))
+        end_pool = ctx.enter_context(tc.tile_pool(name="end", bufs=3))
         tr_psum = ctx.enter_context(tc.psum_pool(name="tr_psum", bufs=3))
         feat_psum = ctx.enter_context(tc.psum_pool(name="feat_psum", bufs=2))
         proj_psum = ctx.enter_context(tc.psum_pool(name="proj_psum", bufs=3))
@@ -80,15 +81,17 @@ def tile_ufoattention_pa_kernel(tc, queries, Wk, bk, Wv, bv, gamma, out):
             )
         load_x(0, 2, 4)
         nc.sync.dma_start(out=w_raw[0][:], in_=Wk.rearrange("(s q e) n -> q s e n", s=2, e=2))
+        load_x(1, 0, 2)
         nc.sync.dma_start(out=w_raw[1][:], in_=Wv.rearrange("(s q e) n -> q s e n", s=2, e=2))
-        for g in range(1, GROUPS):
+        load_x(1, 2, 4)
+        for g in range(2, GROUPS):
             load_x(g, 0, 4)
         gamma_all = consts.tile([P, HEADS], BF16, name="gamma_all")
         nc.sync.dma_start(out=gamma_all[:], in_=gamma.rearrange("a h b c -> (a h b c)").partition_broadcast(P))
 
         xt_grouped = {}
 
-        def turn_x(g, u):
+        def turn_x(g, u, copy=nc.scalar.copy):
             x_words = x_tiles[g][:].bitcast(F32).rearrange("p (j s q) -> p j s q", j=PACK, s=2)
             if u == 0:
                 xt_grouped[g] = xt_pool.tile([P, PACK * K_PASS], BF16, name="xt_grouped", align_bytes=64)
@@ -97,7 +100,7 @@ def tile_ufoattention_pa_kernel(tc, queries, Wk, bk, Wv, bv, gamma, out):
             for e in range(2):
                 for s in range(2):
                     nc.tensor.transpose(bank[:, 2 * e + s, :], x_words[:, 2 * u + e, s, :], ident[:])
-            nc.scalar.copy(out=words[:, u, :, :], in_=bank[:].rearrange("q f p -> q p f"))
+            copy(out=words[:, u, :, :], in_=bank[:].rearrange("q f p -> q p f"))
 
         def quantise_x(g):
             x_codes = xt_pool.tile([P, K_PASS], U32, name="x_codes", align_bytes=64)
@@ -113,9 +116,7 @@ def tile_ufoattention_pa_kernel(tc, queries, Wk, bk, Wv, bv, gamma, out):
                 nc.tensor.matmul(out=idle_bank[:], lhsT=ones[:], rhs=idle_rhs[:], start=True, stop=True)
 
         keep_busy(4)
-        turn_x(0, 0)
-        turn_x(0, 1)
-        keep_busy(5)
+        turn_x(0, 0, nc.vector.tensor_copy)
 
         bias_bank = proj_psum.tile([P, 2, HALF], F32, name="bias_bank", tag="proj_bank")
         for i in range(2):
@@ -132,6 +133,14 @@ def tile_ufoattention_pa_kernel(tc, queries, Wk, bk, Wv, bv, gamma, out):
             nc.tensor.matmul(
                 out=col_bank[:, n, :], lhsT=bias_row[:, lo : lo + P], rhs=ones[:, 0:ONES_COLS], start=True, stop=True
             )
+        bias = consts.tile([P, 2, HALF], F32, name="bias")
+        nc.vector.tensor_copy(out=bias[:], in_=bias_bank[:])
+        bias_col = consts.tile([P, PACK], F32, name="bias_col")
+        nc.scalar.copy(out=bias_col[:], in_=col_bank[:, :, 0])
+
+        turn_x(0, 1)
+        keep_busy(4)
+
         w_codes = consts.tile([P, 2, FEATURES], U32, name="w_codes", align_bytes=64)
         w_scales = consts.tile([P, 2, FEATURES], U8, name="w_scales", align_bytes=64)
         w_grouped = []
@@ -153,11 +162,8 @@ def tile_ufoattention_pa_kernel(tc, queries, Wk, bk, Wv, bv, gamma, out):
 
         regroup_w(nc.vector.tensor_copy, 0, HALF, FEATURES)
         regroup_w(nc.scalar.copy, 0, 0, HALF)
+        turn_x(1, 0)
         quantise_x(0)
-        bias = consts.tile([P, 2, HALF], F32, name="bias")
-        nc.scalar.copy(out=bias[:], in_=bias_bank[:])
-        bias_col = consts.tile([P, PACK], F32, name="bias_col")
-        nc.scalar.copy(out=bias_col[:], in_=col_bank[:, :, 0])
         quantise_w(0, HALF, FEATURES)
         quantise_w(0, 0, HALF)
         regroup_w(nc.vector.tensor_copy, 1, 0, FEATURES)
@@ -170,7 +176,7 @@ def tile_ufoattention_pa_kernel(tc, queries, Wk, bk, Wv, bv, gamma, out):
         feats = {}
 
         def way2_tile(g, n):
-            pair, i = TILES[n]
+            pair, i = TILES[n] if g == 0 else PAIRWISE[n]
             lo = HALF + pair * P
             x_codes, x_scales = xq[g]
             bank = feat_psum.tile([P, K_PASS], F32, name="feat_bank")
@@ -184,11 +190,11 @@ def tile_ufoattention_pa_kernel(tc, queries, Wk, bk, Wv, bv, gamma, out):
                 stop=True,
             )
             feat_sb = feat_pool.tile([P, K_PASS], BF16, name="feat_sb")
-            nc.scalar.activation(out=feat_sb[:], in_=bank[:], func=ACT.Identity, bias=bias_col[:, n : n + 1])
+            nc.scalar.activation(out=feat_sb[:], in_=bank[:], func=ACT.Identity, bias=bias_col[:, 2 * i + pair : 2 * i + pair + 1])
             feats[g, pair, i] = feat_sb
 
         def way1_tile(g, n):
-            pair, i = TILES[n]
+            pair, i = TILES[n] if g == 0 else PAIRWISE[n]
             lo = pair * P
             x_codes, x_scales = xq[g]
             bank = proj_psum.tile([P, PACK, P], F32, name="proj_bank", tag="proj_bank")
@@ -263,10 +269,20 @@ def tile_ufoattention_pa_kernel(tc, queries, Wk, bk, Wv, bv, gamma, out):
             nc.scalar.activation(out=inverse[:], in_=total[:], func=ACT.Abs_reciprocal_sqrt)
             return inverse
 
+        def vector_squares(kv):
+            squares = end_pool.tile([P, HEAD_PAIRS, D_HEAD], F32, name="squares")
+            nc.vector.tensor_tensor(out=squares[:], in0=kv[:], in1=kv[:], op=ALU.mult)
+            return squares
+
+        def vector_sums(squares):
+            total = end_pool.tile([P, HEAD_PAIRS], F32, name="total")
+            nc.vector.tensor_reduce(out=total[:], in_=squares[:], axis=AX.X, op=ALU.add)
+            return total
+
         def end_square(kv):
             pairs = kv.shape[1]
-            squares = end_pool.tile([P, pairs, D_HEAD], F32, name="squares")
-            total = end_pool.tile([P, pairs], F32, name="total")
+            squares = end_pool.tile([P, pairs, D_HEAD], F32, name="low_squares")
+            total = end_pool.tile([P, pairs], F32, name="low_total")
             for i in range(pairs):
                 nc.scalar.activation(
                     out=squares[:, i, :], in_=kv[:, i, :], func=ACT.Square, accum_out=total[:, i : i + 1]
@@ -304,19 +320,14 @@ def tile_ufoattention_pa_kernel(tc, queries, Wk, bk, Wv, bv, gamma, out):
 
             way2_tile(g, 0)
             way1_tile(g, 0)
-            if g == 0:
-                turn_x(1, 0)
             if ending is not None:
                 kv_bank = second_products(ending)
             if storing is not None:
-                total = end_pool.tile([P, HEAD_PAIRS], F32, name="total")
-                nc.vector.tensor_reduce(out=total[:], in_=squares[:], axis=AX.X, op=ALU.add)
+                total = vector_sums(squares)
             way2_tile(g, 1)
             way1_tile(g, 1)
             if ending is not None:
-                kv = end_copy(
-                    kv_bank, 0, HEAD_PAIRS, nc.scalar.copy, nc.scalar.copy if last_end else nc.vector.tensor_copy
-                )
+                kv = end_copy(kv_bank, 0, HEAD_PAIRS, nc.scalar.copy, nc.scalar.copy)
             if storing is not None:
                 inverse = end_inverse(total)
             unit = 2 * g + 3
@@ -326,8 +337,7 @@ def tile_ufoattention_pa_kernel(tc, queries, Wk, bk, Wv, bv, gamma, out):
                 turn_back(g - 1, 1, nc.scalar.copy)
                 codes1[g - 1] = quantise_kv(grouped1[g - 1], "kv1")
             if ending is not None and not last_end:
-                squares = end_pool.tile([P, HEAD_PAIRS, D_HEAD], F32, name="squares")
-                nc.vector.tensor_tensor(out=squares[:], in0=kv[:], in1=kv[:], op=ALU.mult)
+                squares = vector_squares(kv)
             if storing is not None:
                 end_store(storing, 0, kv, inverse)
 
@@ -343,6 +353,8 @@ def tile_ufoattention_pa_kernel(tc, queries, Wk, bk, Wv, bv, gamma, out):
             if unit < 2 * GROUPS:
                 turn_x(unit // 2, unit % 2)
             turn_back(g, 0, nc.scalar.copy)
+            if g == GROUPS - 1:
+                codes1[g] = quantise_kv(grouped1[g], "kv1")
             if g > 0:
                 codes2[g - 1] = quantise_kv(grouped2[g - 1], "kv2")
 
@@ -350,14 +362,12 @@ def tile_ufoattention_pa_kernel(tc, queries, Wk, bk, Wv, bv, gamma, out):
         b = BATCHES - 1
         words = grouped2[g][:].rearrange("p a i f t -> p (a i f t)").bitcast(F32)
         words = words.rearrange("p (a i f u) -> p a i f u", a=WAY_PAIRS, i=2, u=2)
-        codes1[g] = quantise_kv(grouped1[g], "kv1")
         for i in range(2):
             bank = tr_psum.tile([P, 2, P], F32, name="last_bank", tag="tr_bank")
             feat_words = feats[g, 1, i][:].bitcast(F32)
             for u in range(2):
                 nc.tensor.transpose(bank[:, u, :], feat_words[:, u * P : (u + 1) * P], ident[:])
             nc.scalar.copy(out=words[:, 1, i, :, :], in_=bank[:].rearrange("p u f -> p f u"))
-        inverse = end_inverse(end_square(kv))
         kv_bank = proj_psum.tile([P, HEAD_PAIRS, P], F32, name="kv_bank", tag="proj_bank")
         second_product(b, kv_bank, 0)
         codes = kvq_pool.tile([P, WAY_PAIRS, 2, P], U32, name="kv2_codes", align_bytes=64)
@@ -369,14 +379,15 @@ def tile_ufoattention_pa_kernel(tc, queries, Wk, bk, Wv, bv, gamma, out):
                 in_=grouped2[g][:, pair, :, :, :].rearrange("p i f t -> p (i f t)"),
             )
         codes2[g] = (codes, scales)
-        end_store(b - 1, 0, kv, inverse)
+        inverse = end_inverse(end_square(kv))
         kv_low = end_copy(kv_bank, 0, WAY_PAIRS, nc.scalar.copy, nc.scalar.copy)
-        total_low = end_square(kv_low)
-        inverse_low = end_inverse(total_low)
         kv_bank2 = proj_psum.tile([P, HEAD_PAIRS, P], F32, name="kv_bank", tag="proj_bank")
         second_product(b, kv_bank2, 1)
         kv_high = end_copy(kv_bank2, WAY_PAIRS, HEAD_PAIRS, nc.vector.tensor_copy, nc.vector.tensor_copy)
+        total_low = end_square(kv_low)
         total_high = end_square(kv_high)
+        inverse_low = end_inverse(total_low)
         inverse_high = end_inverse(total_high)
+        end_store(b - 1, 0, kv, inverse)
         end_store(b, 0, kv_low, inverse_low)
         end_store(b, WAY_PAIRS, kv_high, inverse_high)

@@ -43,7 +43,7 @@ def tile_ufoattention_pa_kernel(tc, queries, Wk, bk, Wv, bv, gamma, out):
         xt_pool = ctx.enter_context(tc.tile_pool(name="xt", bufs=3))
         kv_pool = ctx.enter_context(tc.tile_pool(name="kv", bufs=2))
         feat_pool = ctx.enter_context(tc.tile_pool(name="feat", bufs=8))
-        kvq_pool = ctx.enter_context(tc.tile_pool(name="kvq", bufs=4))
+        kvq_pool = ctx.enter_context(tc.tile_pool(name="kvq", bufs=6))
         end_pool = ctx.enter_context(tc.tile_pool(name="end", bufs=3))
         tr_psum = ctx.enter_context(tc.psum_pool(name="tr_psum", bufs=3))
         feat_psum = ctx.enter_context(tc.psum_pool(name="feat_psum", bufs=2))
@@ -190,7 +190,12 @@ def tile_ufoattention_pa_kernel(tc, queries, Wk, bk, Wv, bv, gamma, out):
                 stop=True,
             )
             feat_sb = feat_pool.tile([P, K_PASS], BF16, name="feat_sb")
-            nc.scalar.activation(out=feat_sb[:], in_=bank[:], func=ACT.Identity, bias=bias_col[:, 2 * i + pair : 2 * i + pair + 1])
+            if n == 3 and g in (3, 5):
+                nc.vector.tensor_scalar(
+                    out=feat_sb[:], in0=bank[:], scalar1=bias_col[:, 2 * i + pair : 2 * i + pair + 1], scalar2=None, op0=ALU.add
+                )
+            else:
+                nc.scalar.activation(out=feat_sb[:], in_=bank[:], func=ACT.Identity, bias=bias_col[:, 2 * i + pair : 2 * i + pair + 1])
             feats[g, pair, i] = feat_sb
 
         def way1_tile(g, n):
@@ -289,6 +294,27 @@ def tile_ufoattention_pa_kernel(tc, queries, Wk, bk, Wv, bv, gamma, out):
                 )
             return total
 
+        def store_result(b, lo, result):
+            pairs = result.shape[1]
+            nc.sync.dma_start(
+                out=out[b].rearrange("(pair half) i j -> (half i) pair j", half=2)[:, lo : lo + pairs, :], in_=result[:]
+            )
+
+        def end_factor(inverse):
+            factor = end_pool.tile([P, HEAD_PAIRS], F32, name="factor")
+            nc.gpsimd.tensor_tensor(out=factor[:], in0=inverse[:], in1=gain[:], op=ALU.mult)
+            return factor
+
+        def end_store_batch(b, kv, factor):
+            result = end_pool.tile([P, HEAD_PAIRS, D_HEAD], F32, name="result_batch")
+            nc.vector.tensor_tensor(
+                out=result[:],
+                in0=kv[:],
+                in1=factor[:].unsqueeze(2).to_broadcast([P, HEAD_PAIRS, D_HEAD]),
+                op=ALU.mult,
+            )
+            store_result(b, 0, result)
+
         def end_store(b, lo, kv, inverse):
             pairs = kv.shape[1]
             result = end_pool.tile([P, pairs, D_HEAD], F32, name="result")
@@ -301,9 +327,7 @@ def tile_ufoattention_pa_kernel(tc, queries, Wk, bk, Wv, bv, gamma, out):
                     op0=ALU.mult,
                     op1=ALU.mult,
                 )
-            nc.sync.dma_start(
-                out=out[b].rearrange("(pair half) i j -> (half i) pair j", half=2)[:, lo : lo + pairs, :], in_=result[:]
-            )
+            store_result(b, lo, result)
 
         def second_products(b):
             bank = proj_psum.tile([P, HEAD_PAIRS, P], F32, name="kv_bank", tag="proj_bank")
@@ -312,51 +336,54 @@ def tile_ufoattention_pa_kernel(tc, queries, Wk, bk, Wv, bv, gamma, out):
             return bank
 
         for g in range(GROUPS):
-            ending = (g - 3) // 2 if g % 2 == 1 and g > 1 else None
-            storing = (g - 4) // 2 if g % 2 == 0 and g > 2 else None
+            ending = {4: 0, 6: 1, 7: 2}.get(g)
+            storing = {5: 0, 7: 1}.get(g)
             last_end = ending == BATCHES - 2
             grouped1[g] = kv_pool.tile([P, WAY_PAIRS, 2, P, PACK], BF16, name="kv_grouped1", align_bytes=64)
             grouped2[g] = kv_pool.tile([P, WAY_PAIRS, 2, P, PACK], BF16, name="kv_grouped2", align_bytes=64)
 
             way2_tile(g, 0)
             way1_tile(g, 0)
-            if ending is not None:
+            if ending is not None and not last_end:
                 kv_bank = second_products(ending)
             if storing is not None:
                 total = vector_sums(squares)
             way2_tile(g, 1)
             way1_tile(g, 1)
-            if ending is not None:
+            if last_end:
+                kv_bank = second_products(ending)
+                last_kv = end_copy(kv_bank, 0, HEAD_PAIRS, nc.scalar.copy, nc.scalar.copy)
+            elif ending is not None:
                 kv = end_copy(kv_bank, 0, HEAD_PAIRS, nc.scalar.copy, nc.scalar.copy)
             if storing is not None:
-                inverse = end_inverse(total)
+                factor = end_factor(end_inverse(total))
             unit = 2 * g + 3
             if unit < 2 * GROUPS:
                 turn_x(unit // 2, unit % 2)
             if g > 0:
                 turn_back(g - 1, 1, nc.scalar.copy)
                 codes1[g - 1] = quantise_kv(grouped1[g - 1], "kv1")
-            if ending is not None and not last_end:
-                squares = vector_squares(kv)
-            if storing is not None:
-                end_store(storing, 0, kv, inverse)
 
             way2_tile(g, 2)
             way1_tile(g, 2)
             if g + 1 < GROUPS:
                 quantise_x(g + 1)
+            if ending is not None and not last_end:
+                squares = vector_squares(kv)
             if g == 3:
                 load_gain()
+            if storing is not None:
+                end_store_batch(storing, kv, factor)
             way2_tile(g, 3)
             way1_tile(g, 3)
             unit = 2 * g + 4
             if unit < 2 * GROUPS:
                 turn_x(unit // 2, unit % 2)
             turn_back(g, 0, nc.scalar.copy)
-            if g == GROUPS - 1:
-                codes1[g] = quantise_kv(grouped1[g], "kv1")
             if g > 0:
                 codes2[g - 1] = quantise_kv(grouped2[g - 1], "kv2")
+            if g == GROUPS - 1:
+                codes1[g] = quantise_kv(grouped1[g], "kv1")
 
         g = GROUPS - 1
         b = BATCHES - 1
@@ -379,7 +406,7 @@ def tile_ufoattention_pa_kernel(tc, queries, Wk, bk, Wv, bv, gamma, out):
                 in_=grouped2[g][:, pair, :, :, :].rearrange("p i f t -> p (i f t)"),
             )
         codes2[g] = (codes, scales)
-        inverse = end_inverse(end_square(kv))
+        factor = end_factor(end_inverse(end_square(last_kv)))
         kv_low = end_copy(kv_bank, 0, WAY_PAIRS, nc.scalar.copy, nc.scalar.copy)
         kv_bank2 = proj_psum.tile([P, HEAD_PAIRS, P], F32, name="kv_bank", tag="proj_bank")
         second_product(b, kv_bank2, 1)
@@ -388,6 +415,6 @@ def tile_ufoattention_pa_kernel(tc, queries, Wk, bk, Wv, bv, gamma, out):
         total_high = end_square(kv_high)
         inverse_low = end_inverse(total_low)
         inverse_high = end_inverse(total_high)
-        end_store(b - 1, 0, kv, inverse)
+        end_store_batch(b - 1, last_kv, factor)
         end_store(b, 0, kv_low, inverse_low)
         end_store(b, WAY_PAIRS, kv_high, inverse_high)

@@ -40,7 +40,7 @@ def tile_ufoattention_pa_kernel(tc, queries, Wk, bk, Wv, bv, gamma, out):
     with ExitStack() as ctx:
         consts = ctx.enter_context(tc.tile_pool(name="consts", bufs=1))
         x_pool = ctx.enter_context(tc.tile_pool(name="x", bufs=GROUPS))
-        xt_pool = ctx.enter_context(tc.tile_pool(name="xt", bufs=3))
+        xt_pool = ctx.enter_context(tc.tile_pool(name="xt", bufs=4))
         kv_pool = ctx.enter_context(tc.tile_pool(name="kv", bufs=2))
         feat_pool = ctx.enter_context(tc.tile_pool(name="feat", bufs=8))
         kvq_pool = ctx.enter_context(tc.tile_pool(name="kvq", bufs=6))
@@ -166,8 +166,11 @@ def tile_ufoattention_pa_kernel(tc, queries, Wk, bk, Wv, bv, gamma, out):
         quantise_x(0)
         quantise_w(0, HALF, FEATURES)
         quantise_w(0, 0, HALF)
-        regroup_w(nc.vector.tensor_copy, 1, 0, FEATURES)
-        quantise_w(1, 0, FEATURES)
+        regroup_w(nc.scalar.copy, 1, 0, P)
+        regroup_w(nc.vector.tensor_copy, 1, HALF, FEATURES)
+        regroup_w(nc.vector.tensor_copy, 1, P, HALF)
+        quantise_w(1, HALF, FEATURES)
+        quantise_w(1, 0, HALF)
 
         grouped1 = {}
         grouped2 = {}
@@ -190,7 +193,7 @@ def tile_ufoattention_pa_kernel(tc, queries, Wk, bk, Wv, bv, gamma, out):
                 stop=True,
             )
             feat_sb = feat_pool.tile([P, K_PASS], BF16, name="feat_sb")
-            if n == 3 and g in (3, 5):
+            if n == 1 and g in (1, 3, 5):
                 nc.vector.tensor_scalar(
                     out=feat_sb[:], in0=bank[:], scalar1=bias_col[:, 2 * i + pair : 2 * i + pair + 1], scalar2=None, op0=ALU.add
                 )
@@ -357,17 +360,17 @@ def tile_ufoattention_pa_kernel(tc, queries, Wk, bk, Wv, bv, gamma, out):
                 kv = end_copy(kv_bank, 0, HEAD_PAIRS, nc.scalar.copy, nc.scalar.copy)
             if storing is not None:
                 factor = end_factor(end_inverse(total))
-            unit = 2 * g + 3
-            if unit < 2 * GROUPS:
-                turn_x(unit // 2, unit % 2)
+            for unit in (3, 4) if g == 0 else (2 * g + 4,):
+                if unit < 2 * GROUPS:
+                    turn_x(unit // 2, unit % 2)
             if g > 0:
                 turn_back(g - 1, 1, nc.scalar.copy)
                 codes1[g - 1] = quantise_kv(grouped1[g - 1], "kv1")
 
-            way2_tile(g, 2)
-            way1_tile(g, 2)
             if g + 1 < GROUPS:
                 quantise_x(g + 1)
+            way2_tile(g, 2)
+            way1_tile(g, 2)
             if ending is not None and not last_end:
                 squares = vector_squares(kv)
             if g == 3:
@@ -376,7 +379,7 @@ def tile_ufoattention_pa_kernel(tc, queries, Wk, bk, Wv, bv, gamma, out):
                 end_store_batch(storing, kv, factor)
             way2_tile(g, 3)
             way1_tile(g, 3)
-            unit = 2 * g + 4
+            unit = 2 * g + 5
             if unit < 2 * GROUPS:
                 turn_x(unit // 2, unit % 2)
             turn_back(g, 0, nc.scalar.copy)

@@ -50,10 +50,10 @@ def tile_ufoattention_pa_kernel(tc, queries, Wk, bk, Wv, bv, gamma, out):
         proj_psum = ctx.enter_context(tc.psum_pool(name="proj_psum", bufs=3))
         ctx.enter_context(tc.manual_schedule())
 
-        warm = consts.tile([P, 1], F32, name="warm")
-        nc.vector.memset(warm[:], 1.0)
         bias_row = consts.tile([P, 2 * FEATURES], BF16, name="bias_row")
         nc.vector.memset(bias_row[:], 0.0)
+        warm = consts.tile([P, 1], F32, name="warm")
+        nc.vector.memset(warm[:], 1.0)
         ones = consts.tile([P, P], BF16, name="ones")
         nc.vector.memset(ones[:], 1.0)
         idle_rhs = consts.tile([P, FEATURES], BF16, name="idle_rhs")
@@ -75,11 +75,11 @@ def tile_ufoattention_pa_kernel(tc, queries, Wk, bk, Wv, bv, gamma, out):
             )
 
         load_x(0, 0, 2)
+        load_x(0, 2, 4)
         for i, b_vec in enumerate((bk, bv)):
             nc.sync.dma_start(
                 out=bias_row[0:1, i * FEATURES : (i + 1) * FEATURES], in_=b_vec.rearrange("(o n) -> o n", o=1)
             )
-        load_x(0, 2, 4)
         nc.sync.dma_start(out=w_raw[0][:], in_=Wk.rearrange("(s q e) n -> q s e n", s=2, e=2))
         load_x(1, 0, 2)
         nc.sync.dma_start(out=w_raw[1][:], in_=Wv.rearrange("(s q e) n -> q s e n", s=2, e=2))
@@ -117,6 +117,7 @@ def tile_ufoattention_pa_kernel(tc, queries, Wk, bk, Wv, bv, gamma, out):
 
         keep_busy(4)
         turn_x(0, 0, nc.vector.tensor_copy)
+        turn_x(0, 1)
 
         bias_bank = proj_psum.tile([P, 2, HALF], F32, name="bias_bank", tag="proj_bank")
         for i in range(2):
@@ -138,7 +139,6 @@ def tile_ufoattention_pa_kernel(tc, queries, Wk, bk, Wv, bv, gamma, out):
         bias_col = consts.tile([P, PACK], F32, name="bias_col")
         nc.scalar.copy(out=bias_col[:], in_=col_bank[:, :, 0])
 
-        turn_x(0, 1)
         keep_busy(4)
 
         w_codes = consts.tile([P, 2, FEATURES], U32, name="w_codes", align_bytes=64)
@@ -193,7 +193,7 @@ def tile_ufoattention_pa_kernel(tc, queries, Wk, bk, Wv, bv, gamma, out):
                 stop=True,
             )
             feat_sb = feat_pool.tile([P, K_PASS], BF16, name="feat_sb")
-            if n == 1 and g in (1, 3, 5):
+            if n == 1 and g in (1, 3):
                 nc.vector.tensor_scalar(
                     out=feat_sb[:], in0=bank[:], scalar1=bias_col[:, 2 * i + pair : 2 * i + pair + 1], scalar2=None, op0=ALU.add
                 )

from contextlib import ExitStack

import concourse.mybir as mybir
from concourse.masks import make_identity

F32 = mybir.dt.float32
BF16 = mybir.dt.bfloat16
U32 = mybir.dt.uint32
U8 = mybir.dt.uint8
FP8X4 = mybir.dt.float8_e4m3fn_x4
ACT = mybir.ActivationFunctionType
ALU = mybir.AluOpType
AX = mybir.AxisListType

P = 128
PACK = 4
K_PASS = P * PACK

BATCHES = 4
TOKENS = 1024
D_MODEL = 512
HEADS = 8
D_HEAD = 64
FEATURES = HEADS * D_HEAD

GROUPS = BATCHES * TOKENS // K_PASS
HEAD_PAIRS = FEATURES // P
WAY_PAIRS = HEAD_PAIRS // 2
HALF = FEATURES // 2
ONES_COLS = 32

FLOPS = 2 * BATCHES * TOKENS * D_MODEL * 2 * FEATURES + 2 * BATCHES * HEADS * TOKENS * D_HEAD * D_HEAD

TILES = [(0, 0), (1, 0), (0, 1), (1, 1)]
PAIRWISE = [(0, 0), (0, 1), (1, 0), (1, 1)]


def tile_ufoattention_pa_kernel(tc, queries, Wk, bk, Wv, bv, gamma, out):
    nc = tc.nc
    with ExitStack() as ctx:
        consts = ctx.enter_context(tc.tile_pool(name="consts", bufs=1))
        x_pool = ctx.enter_context(tc.tile_pool(name="x", bufs=GROUPS))
        xt_pool = ctx.enter_context(tc.tile_pool(name="xt", bufs=4))
        kv_pool = ctx.enter_context(tc.tile_pool(name="kv", bufs=2))
        feat_pool = ctx.enter_context(tc.tile_pool(name="feat", bufs=8))
        kvq_pool = ctx.enter_context(tc.tile_pool(name="kvq", bufs=6))
        end_pool = ctx.enter_context(tc.tile_pool(name="end", bufs=3))
        tr_psum = ctx.enter_context(tc.psum_pool(name="tr_psum", bufs=3))
        feat_psum = ctx.enter_context(tc.psum_pool(name="feat_psum", bufs=2))
        proj_psum = ctx.enter_context(tc.psum_pool(name="proj_psum", bufs=3))
        ctx.enter_context(tc.manual_schedule())

        bias_row = consts.tile([P, 2 * FEATURES], BF16, name="bias_row")
        nc.vector.memset(bias_row[:], 0.0)
        warm = consts.tile([P, 1], F32, name="warm")
        nc.vector.memset(warm[:], 1.0)
        ones = consts.tile([P, P], BF16, name="ones")
        nc.vector.memset(ones[:], 1.0)
        idle_rhs = consts.tile([P, FEATURES], BF16, name="idle_rhs")
        nc.vector.memset(idle_rhs[:], 0.0)
        ident = consts.tile([P, P], F32, name="ident")
        make_identity(nc, ident[:])
        nc.scalar.activation(out=warm[:], in_=warm[:], func=ACT.Abs_reciprocal_sqrt)
        x_groups = queries.flatten_outer_dims().rearrange("(g p j) d -> g p (j d)", p=P, j=PACK)
        x_tiles = []
        for g in range(GROUPS):
            x_tiles.append(x_pool.tile([P, PACK * D_MODEL], BF16, name="x_sb"))
        w_raw = []
        for w_name in ("wk_raw", "wv_raw"):
            w_raw.append(consts.tile([P, 2, 2, FEATURES], BF16, name=w_name))

        def load_x(g, lo, hi):
            nc.sync.dma_start(
                out=x_tiles[g][:, lo * D_MODEL : hi * D_MODEL], in_=x_groups[g][:, lo * D_MODEL : hi * D_MODEL]
            )

        load_x(0, 0, 2)
        load_x(0, 2, 4)
        for i, b_vec in enumerate((bk, bv)):
            nc.sync.dma_start(
                out=bias_row[0:1, i * FEATURES : (i + 1) * FEATURES], in_=b_vec.rearrange("(o n) -> o n", o=1)
            )
        nc.sync.dma_start(out=w_raw[0][:], in_=Wk.rearrange("(s q e) n -> q s e n", s=2, e=2))
        load_x(1, 0, 2)
        nc.sync.dma_start(out=w_raw[1][:], in_=Wv.rearrange("(s q e) n -> q s e n", s=2, e=2))
        load_x(1, 2, 4)
        for g in range(2, GROUPS):
            load_x(g, 0, 4)
        gamma_all = consts.tile([P, HEADS], BF16, name="gamma_all")
        nc.sync.dma_start(out=gamma_all[:], in_=gamma.rearrange("a h b c -> (a h b c)").partition_broadcast(P))

        xt_grouped = {}

        def turn_x(g, u, copy=nc.scalar.copy):
            x_words = x_tiles[g][:].bitcast(F32).rearrange("p (j s q) -> p j s q", j=PACK, s=2)
            if u == 0:
                xt_grouped[g] = xt_pool.tile([P, PACK * K_PASS], BF16, name="xt_grouped", align_bytes=64)
            words = xt_grouped[g][:].bitcast(F32).rearrange("q (u p f) -> q u p f", u=2, f=PACK)
            bank = tr_psum.tile([P, PACK, P], F32, name="xt_bank", tag="tr_bank")
            for e in range(2):
                for s in range(2):
                    nc.tensor.transpose(bank[:, 2 * e + s, :], x_words[:, 2 * u + e, s, :], ident[:])
            copy(out=words[:, u, :, :], in_=bank[:].rearrange("q f p -> q p f"))

        def quantise_x(g):
            x_codes = xt_pool.tile([P, K_PASS], U32, name="x_codes", align_bytes=64)
            x_scales = xt_pool.tile([P, K_PASS], U8, name="x_scales", align_bytes=64)
            nc.vector.quantize_mx(out=x_codes[:].bitcast(FP8X4), scales=x_scales[:], in_=xt_grouped[g][:])
            xq[g] = (x_codes, x_scales)

        xq = {}

        def keep_busy(count):
            idle_bank = proj_psum.tile([P, FEATURES], F32, name="idle_bank", tag="proj_bank")
            for i in range(count):
                nc.tensor.matmul(out=idle_bank[:], lhsT=ones[:], rhs=idle_rhs[:], start=True, stop=True)

        keep_busy(4)
        turn_x(0, 0, nc.vector.tensor_copy)
        turn_x(0, 1)

        bias_bank = proj_psum.tile([P, 2, HALF], F32, name="bias_bank", tag="proj_bank")
        for i in range(2):
            nc.tensor.matmul(
                out=bias_bank[:, i, :],
                lhsT=ones[:],
                rhs=bias_row[:, i * FEATURES : i * FEATURES + HALF],
                start=True,
                stop=True,
            )
        col_bank = proj_psum.tile([P, PACK, ONES_COLS], F32, name="col_bank", tag="proj_bank")
        for n, (pair, i) in enumerate(TILES):
            lo = i * FEATURES + HALF + pair * P
            nc.tensor.matmul(
                out=col_bank[:, n, :], lhsT=bias_row[:, lo : lo + P], rhs=ones[:, 0:ONES_COLS], start=True, stop=True
            )
        bias = consts.tile([P, 2, HALF], F32, name="bias")
        nc.vector.tensor_copy(out=bias[:], in_=bias_bank[:])
        bias_col = consts.tile([P, PACK], F32, name="bias_col")
        nc.scalar.copy(out=bias_col[:], in_=col_bank[:, :, 0])

        keep_busy(4)

        w_codes = consts.tile([P, 2, FEATURES], U32, name="w_codes", align_bytes=64)
        w_scales = consts.tile([P, 2, FEATURES], U8, name="w_scales", align_bytes=64)
        w_grouped = []
        for i, w_name in enumerate(("wk_grouped", "wv_grouped")):
            w_grouped.append(consts.tile([P, FEATURES, PACK], BF16, name=w_name, align_bytes=64))

        def regroup_w(copy, i, lo, hi):
            copy(
                out=w_grouped[i][:, lo:hi, :].rearrange("p (c i) t -> p c t i", i=PACK),
                in_=w_raw[i][:].rearrange("p s e n -> p (s e) n")[:, :, lo:hi].rearrange("p t (c i) -> p c t i", i=PACK),
            )

        def quantise_w(i, lo, hi):
            nc.vector.quantize_mx(
                out=w_codes[:, i, lo:hi].bitcast(FP8X4),
                scales=w_scales[:, i, lo:hi],
                in_=w_grouped[i][:, lo:hi, :].rearrange("p n t -> p (n t)"),
            )

        regroup_w(nc.vector.tensor_copy, 0, HALF, FEATURES)
        regroup_w(nc.scalar.copy, 0, 0, HALF)
        turn_x(1, 0)
        quantise_x(0)
        quantise_w(0, HALF, FEATURES)
        quantise_w(0, 0, HALF)
        regroup_w(nc.scalar.copy, 1, 0, P)
        regroup_w(nc.vector.tensor_copy, 1, HALF, FEATURES)
        regroup_w(nc.vector.tensor_copy, 1, P, HALF)
        quantise_w(1, HALF, FEATURES)
        quantise_w(1, 0, HALF)

        grouped1 = {}
        grouped2 = {}
        codes1 = {}
        codes2 = {}
        feats = {}

        def way2_tile(g, n):
            pair, i = TILES[n] if g == 0 else PAIRWISE[n]
            lo = HALF + pair * P
            x_codes, x_scales = xq[g]
            bank = feat_psum.tile([P, K_PASS], F32, name="feat_bank")
            nc.tensor.matmul_mx(
                out=bank[:],
                lhsT=w_codes[:, i, lo : lo + P].bitcast(FP8X4),
                lhsT_scale=w_scales[:, i, lo : lo + P],
                rhs=x_codes[:].bitcast(FP8X4),
                rhs_scale=x_scales[:],
                start=True,
                stop=True,
            )
            feat_sb = feat_pool.tile([P, K_PASS], BF16, name="feat_sb")
            if n == 1 and g in (1, 3):
                nc.vector.tensor_scalar(
                    out=feat_sb[:], in0=bank[:], scalar1=bias_col[:, 2 * i + pair : 2 * i + pair + 1], scalar2=None, op0=ALU.add
                )
            else:
                nc.scalar.activation(out=feat_sb[:], in_=bank[:], func=ACT.Identity, bias=bias_col[:, 2 * i + pair : 2 * i + pair + 1])
            feats[g, pair, i] = feat_sb

        def way1_tile(g, n):
            pair, i = TILES[n] if g == 0 else PAIRWISE[n]
            lo = pair * P
            x_codes, x_scales = xq[g]
            bank = proj_psum.tile([P, PACK, P], F32, name="proj_bank", tag="proj_bank")
            for j in range(PACK):
                cols = slice(j * P, (j + 1) * P)
                nc.tensor.matmul_mx(
                    out=bank[:, j, :],
                    lhsT=x_codes[:, cols].bitcast(FP8X4),
                    lhsT_scale=x_scales[:, cols],
                    rhs=w_codes[:, i, lo : lo + P].bitcast(FP8X4),
                    rhs_scale=w_scales[:, i, lo : lo + P],
                    start=True,
                    stop=True,
                )
            nc.vector.tensor_tensor(
                out=grouped1[g][:, pair, i, :, :],
                in0=bank[:].rearrange("p j w -> p w j"),
                in1=bias[:, i, lo : lo + P].unsqueeze(2).to_broadcast([P, P, PACK]),
                op=ALU.add,
            )

        def turn_back(g, pair, copy):
            bank = tr_psum.tile([P, 2, 2, P], F32, name="tok_bank", tag="tr_bank")
            for i in range(2):
                words = feats[g, pair, i][:].bitcast(F32)
                for u in range(2):
                    nc.tensor.transpose(bank[:, i, u, :], words[:, u * P : (u + 1) * P], ident[:])
            words = grouped2[g][:].rearrange("p a i f t -> p (a i f t)").bitcast(F32)
            words = words.rearrange("p (a i f u) -> p a i f u", a=WAY_PAIRS, i=2, u=2)
            copy(out=words[:, pair, :, :, :], in_=bank[:].rearrange("p i u f -> p i f u"))

        def quantise_kv(grouped, name):
            codes = kvq_pool.tile([P, WAY_PAIRS, 2, P], U32, name=name + "_codes", align_bytes=64)
            scales = kvq_pool.tile([P, WAY_PAIRS, 2, P], U8, name=name + "_scales", align_bytes=64)
            nc.vector.quantize_mx(
                out=codes[:].rearrange("p a i f -> p (a i f)").bitcast(FP8X4),
                scales=scales[:].rearrange("p a i f -> p (a i f)"),
                in_=grouped[:].rearrange("p a i f t -> p (a i f t)"),
            )
            return codes, scales

        def second_product(b, kv_bank, half):
            store = (codes1, codes2)[half]
            for pair in range(WAY_PAIRS):
                for c in range(2):
                    codes, scales = store[2 * b + c]
                    nc.tensor.matmul_mx(
                        out=kv_bank[:, 2 * half + pair, :],
                        lhsT=codes[:, pair, 0, :].bitcast(FP8X4),
                        lhsT_scale=scales[:, pair, 0, :],
                        rhs=codes[:, pair, 1, :].bitcast(FP8X4),
                        rhs_scale=scales[:, pair, 1, :],
                        start=(c == 0),
                        stop=(c == 1),
                    )

        gain = consts.tile([P, HEAD_PAIRS], F32, name="gain")

        def load_gain():
            gamma_by_half = gamma_all[:].rearrange("p (pair half) -> p half pair", half=2)
            nc.gpsimd.tensor_copy(out=gain[0:D_HEAD, :], in_=gamma_by_half[0:D_HEAD, 0, :])
            nc.gpsimd.tensor_copy(out=gain[D_HEAD:P, :], in_=gamma_by_half[D_HEAD:P, 1, :])

        def end_copy(kv_bank, lo, hi, copy_low, copy_high):
            kv = end_pool.tile([P, hi - lo, D_HEAD], F32, name="kv")
            copy_low(out=kv[0:D_HEAD, :, :], in_=kv_bank[0:D_HEAD, lo:hi, 0:D_HEAD])
            copy_high(out=kv[D_HEAD:P, :, :], in_=kv_bank[D_HEAD:P, lo:hi, D_HEAD:P])
            return kv

        def end_inverse(total):
            inverse = end_pool.tile([P, total.shape[1]], F32, name="inverse")
            nc.scalar.activation(out=inverse[:], in_=total[:], func=ACT.Abs_reciprocal_sqrt)
            return inverse

        def vector_squares(kv):
            squares = end_pool.tile([P, HEAD_PAIRS, D_HEAD], F32, name="squares")
            nc.vector.tensor_tensor(out=squares[:], in0=kv[:], in1=kv[:], op=ALU.mult)
            return squares

        def vector_sums(squares):
            total = end_pool.tile([P, HEAD_PAIRS], F32, name="total")
            nc.vector.tensor_reduce(out=total[:], in_=squares[:], axis=AX.X, op=ALU.add)
            return total

        def end_square(kv):
            pairs = kv.shape[1]
            squares = end_pool.tile([P, pairs, D_HEAD], F32, name="low_squares")
            total = end_pool.tile([P, pairs], F32, name="low_total")
            for i in range(pairs):
                nc.scalar.activation(
                    out=squares[:, i, :], in_=kv[:, i, :], func=ACT.Square, accum_out=total[:, i : i + 1]
                )
            return total

        def store_result(b, lo, result):
            pairs = result.shape[1]
            nc.sync.dma_start(
                out=out[b].rearrange("(pair half) i j -> (half i) pair j", half=2)[:, lo : lo + pairs, :], in_=result[:]
            )

        def end_factor(inverse):
            factor = end_pool.tile([P, HEAD_PAIRS], F32, name="factor")
            nc.gpsimd.tensor_tensor(out=factor[:], in0=inverse[:], in1=gain[:], op=ALU.mult)
            return factor

        def end_store_batch(b, kv, factor):
            result = end_pool.tile([P, HEAD_PAIRS, D_HEAD], F32, name="result_batch")
            nc.vector.tensor_tensor(
                out=result[:],
                in0=kv[:],
                in1=factor[:].unsqueeze(2).to_broadcast([P, HEAD_PAIRS, D_HEAD]),
                op=ALU.mult,
            )
            store_result(b, 0, result)

        def end_store(b, lo, kv, inverse):
            pairs = kv.shape[1]
            result = end_pool.tile([P, pairs, D_HEAD], F32, name="result")
            for i in range(pairs):
                nc.vector.tensor_scalar(
                    out=result[:, i, :],
                    in0=kv[:, i, :],
                    scalar1=inverse[:, i : i + 1],
                    scalar2=gain[:, lo + i : lo + i + 1],
                    op0=ALU.mult,
                    op1=ALU.mult,
                )
            store_result(b, lo, result)

        def second_products(b):
            bank = proj_psum.tile([P, HEAD_PAIRS, P], F32, name="kv_bank", tag="proj_bank")
            second_product(b, bank, 0)
            second_product(b, bank, 1)
            return bank

        for g in range(GROUPS):
            ending = {4: 0, 6: 1, 7: 2}.get(g)
            storing = {5: 0, 7: 1}.get(g)
            last_end = ending == BATCHES - 2
            grouped1[g] = kv_pool.tile([P, WAY_PAIRS, 2, P, PACK], BF16, name="kv_grouped1", align_bytes=64)
            grouped2[g] = kv_pool.tile([P, WAY_PAIRS, 2, P, PACK], BF16, name="kv_grouped2", align_bytes=64)

            way2_tile(g, 0)
            way1_tile(g, 0)
            if ending is not None and not last_end:
                kv_bank = second_products(ending)
            if storing is not None:
                total = vector_sums(squares)
            way2_tile(g, 1)
            way1_tile(g, 1)
            if last_end:
                kv_bank = second_products(ending)
                last_kv = end_copy(kv_bank, 0, HEAD_PAIRS, nc.scalar.copy, nc.scalar.copy)
            elif ending is not None:
                kv = end_copy(kv_bank, 0, HEAD_PAIRS, nc.scalar.copy, nc.scalar.copy)
            if storing is not None:
                factor = end_factor(end_inverse(total))
            for unit in (3, 4) if g == 0 else (2 * g + 4,):
                if unit < 2 * GROUPS:
                    turn_x(unit // 2, unit % 2)
            if g > 0:
                turn_back(g - 1, 1, nc.scalar.copy)
                codes1[g - 1] = quantise_kv(grouped1[g - 1], "kv1")

            if g + 1 < GROUPS:
                quantise_x(g + 1)
            way2_tile(g, 2)
            way1_tile(g, 2)
            if ending is not None and not last_end:
                squares = vector_squares(kv)
            if g == 3:
                load_gain()
            if storing is not None:
                end_store_batch(storing, kv, factor)
            way2_tile(g, 3)
            way1_tile(g, 3)
            unit = 2 * g + 5
            if unit < 2 * GROUPS:
                turn_x(unit // 2, unit % 2)
            turn_back(g, 0, nc.scalar.copy)
            if g > 0:
                codes2[g - 1] = quantise_kv(grouped2[g - 1], "kv2")
            if g == GROUPS - 1:
                codes1[g] = quantise_kv(grouped1[g], "kv1")

        g = GROUPS - 1
        b = BATCHES - 1
        words = grouped2[g][:].rearrange("p a i f t -> p (a i f t)").bitcast(F32)
        words = words.rearrange("p (a i f u) -> p a i f u", a=WAY_PAIRS, i=2, u=2)
        for i in range(2):
            bank = tr_psum.tile([P, 2, P], F32, name="last_bank", tag="tr_bank")
            feat_words = feats[g, 1, i][:].bitcast(F32)
            for u in range(2):
                nc.tensor.transpose(bank[:, u, :], feat_words[:, u * P : (u + 1) * P], ident[:])
            nc.scalar.copy(out=words[:, 1, i, :, :], in_=bank[:].rearrange("p u f -> p f u"))
        kv_bank = proj_psum.tile([P, HEAD_PAIRS, P], F32, name="kv_bank", tag="proj_bank")
        second_product(b, kv_bank, 0)
        codes = kvq_pool.tile([P, WAY_PAIRS, 2, P], U32, name="kv2_codes", align_bytes=64)
        scales = kvq_pool.tile([P, WAY_PAIRS, 2, P], U8, name="kv2_scales", align_bytes=64)
        for pair in range(WAY_PAIRS):
            nc.vector.quantize_mx(
                out=codes[:, pair, :, :].rearrange("p i f -> p (i f)").bitcast(FP8X4),
                scales=scales[:, pair, :, :].rearrange("p i f -> p (i f)"),
                in_=grouped2[g][:, pair, :, :, :].rearrange("p i f t -> p (i f t)"),
            )
        codes2[g] = (codes, scales)
        factor = end_factor(end_inverse(end_square(last_kv)))
        kv_low = end_copy(kv_bank, 0, WAY_PAIRS, nc.scalar.copy, nc.scalar.copy)
        kv_bank2 = proj_psum.tile([P, HEAD_PAIRS, P], F32, name="kv_bank", tag="proj_bank")
        second_product(b, kv_bank2, 1)
        kv_high = end_copy(kv_bank2, WAY_PAIRS, HEAD_PAIRS, nc.vector.tensor_copy, nc.vector.tensor_copy)
        total_low = end_square(kv_low)
        total_high = end_square(kv_high)
        inverse_low = end_inverse(total_low)
        inverse_high = end_inverse(total_high)
        end_store_batch(b - 1, last_kv, factor)
        end_store(b, 0, kv_low, inverse_low)
        end_store(b, WAY_PAIRS, kv_high, inverse_high)
